import numpy as np
import ml_dtypes


def mxq(x, axis, fmt="e4m3"):
    dtype, down = {"e4m3": (ml_dtypes.float8_e4m3fn, 7), "e5m2": (ml_dtypes.float8_e5m2, 14)}[fmt]
    v = np.moveaxis(np.asarray(x, np.float32).astype(ml_dtypes.bfloat16).astype(np.float64), axis, -1)
    blocks = v.reshape(v.shape[:-1] + (-1, 32))
    amax = np.abs(blocks).max(-1, keepdims=True)
    byte = np.maximum(np.where(amax > 0, np.frexp(amax)[1] - 1 + 127, 0) - down, 1)
    scale = np.exp2(byte - 127.0)
    codes = (blocks / scale).astype(np.float32).astype(dtype).astype(np.float64)
    return np.moveaxis((codes * scale).reshape(v.shape), -1, axis)


WIDE = False


def mx_kscale(k):
    if not WIDE:
        return np.ones(k)
    levels = np.array([10, -10, 5, -5, 0])
    a = np.random.permutation(np.resize(levels, k // 512 * 4)).reshape(k // 512, 4)
    idx = np.arange(k)
    return np.exp2(a[idx // 512, idx % 128 // 32])


BF16 = ml_dtypes.bfloat16


def bf(x):
    return np.asarray(x, np.float32).astype(BF16)


def f64(x):
    return np.asarray(x).astype(np.float64)


B, N, H, R, L = 8, 512, 512, 2, 2
NEG_INF = -1e30


def setup_inputs():
    s = mx_kscale(H)
    return {"adj": bf(np.random.uniform(size=(B, N, N, R)) * 4.0),
            "x": bf(np.random.standard_normal((B, N, H)) * s),
            "dmask": bf(np.random.uniform(size=(B, 1, N)) > 0.1),
            "W": bf(np.random.standard_normal((R, H, H)) * 1.5 / np.sqrt(H) / s[:, None])}


def reference(adj, x, dmask, W):
    a = f64(adj).transpose(0, 3, 1, 2)
    m = f64(dmask)[:, None, :, :]
    logits = a * m + (1.0 - m) * NEG_INF
    e = np.exp(logits - logits.max(-1, keepdims=True))
    att = e / e.sum(-1, keepdims=True)
    h = mxq(f64(x), 2, "e4m3")[:, None] @ mxq(f64(W), 1, "e4m3")[None]
    g = np.maximum(mxq(att, 3, "e4m3") @ mxq(h, 2, "e4m3"), 0.0)
    return g.sum(1)

@@ -1,0 +1,415 @@
+from contextlib import ExitStack
+
+import concourse.mybir as mybir
+from concourse.masks import make_identity
+
+F32 = mybir.dt.float32
+BF16 = mybir.dt.bfloat16
+U32 = mybir.dt.uint32
+U8 = mybir.dt.uint8
+FP8X4 = mybir.dt.float8_e4m3fn_x4
+ALU = mybir.AluOpType
+ACT = mybir.ActivationFunctionType
+AX = mybir.AxisListType
+
+B, N, H, R = 8, 512, 512, 2
+P = 128
+NT = N // P
+FLOPS = 2 * 2 * B * R * N * N * H
+
+BIG = 3.3895313892515355e38
+NEG = -1e30
+
+
+def tile_rgat_pa_t_kernel(tc, adj, x, dmask, W, out):
+    nc = tc.nc
+    with ExitStack() as ctx:
+        ctx.enter_context(tc.manual_schedule())
+        const = ctx.enter_context(tc.tile_pool(name="const", bufs=1))
+        one = ctx.enter_context(tc.tile_pool(name="one", bufs=1))
+        two = ctx.enter_context(tc.tile_pool(name="two", bufs=2))
+        three = ctx.enter_context(tc.tile_pool(name="three", bufs=3))
+        four = ctx.enter_context(tc.tile_pool(name="four", bufs=4))
+        ps_t = ctx.enter_context(tc.psum_pool(name="ps_t", bufs=2))
+        ps_h = ctx.enter_context(tc.psum_pool(name="ps_h", bufs=2))
+        ps_g = ctx.enter_context(tc.psum_pool(name="ps_g", bufs=2))
+
+        st = [dict() for b in range(B)]
+
+        ident_f = const.tile([P, P], F32)
+        ident_b = const.tile([P, P], BF16)
+        dm = const.tile([P, B * N], BF16)
+        w_codes = const.tile([P, R, H], U32, align_bytes=64)
+        w_scales = const.tile([P, R, H], U8, align_bytes=64)
+        w_stage = two.tile([P, 2, R, 4 * H], BF16, tag="e", align_bytes=64)
+        w_raw = w_stage[:, 0]
+        w_grp = w_stage[:, 1]
+        dm_row = dmask.rearrange("b o m -> (b o m)")
+
+        def load_mask(lo, hi):
+            nc.scalar.dma_start(out=dm[:, lo:hi], in_=dm_row[lo:hi].partition_broadcast(P))
+
+        def load_w(r):
+            for u in range(2):
+                nc.sync.dma_start(
+                    out=w_raw[:, r, 1024 * u : 1024 * u + 1024],
+                    in_=W[r, 256 * u : 256 * u + 256, :].rearrange("(q e) o -> q (e o)", e=2),
+                )
+
+        def load_x(b):
+            xs = three.tile([P, NT * H], BF16, name="xs")
+            nc.sync.dma_start(out=xs[:].rearrange("p (c f) -> p c f", c=NT), in_=x[b].rearrange("(c p) f -> p c f", p=P))
+            st[b]["xs"] = xs
+
+        def load_a(b, pieces):
+            a = three.tile([P, NT, N * R], BF16, name="a")
+            src = adj[b].rearrange("(p t) m r -> p t (m r)", t=NT)
+            step = NT // pieces
+            for k in range(pieces):
+                nc.sync.dma_start(out=a[:, step * k : step * k + step, :], in_=src[:, step * k : step * k + step, :])
+            st[b]["a"] = a
+
+        def make_cap(b, eng):
+            cap = three.tile([P, N, R], BF16, name="cap")
+            eng.tensor_scalar(
+                out=cap[:],
+                in0=dm[:, N * b : N * b + N].unsqueeze(2).to_broadcast([P, N, R]),
+                scalar1=BIG + 1e30,
+                scalar2=NEG,
+                op0=ALU.mult,
+                op1=ALU.add,
+            )
+            st[b]["cap"] = cap
+
+        def w_group(r):
+            nc.vector.tensor_copy(
+                out=w_grp[:, r].rearrange("p (c i t) -> p c t i", i=4, t=4),
+                in_=w_raw[:, r].rearrange("p (t c i) -> p c t i", t=4, i=4),
+            )
+
+        def w_quant(r):
+            nc.vector.quantize_mx(out=w_codes[:, r, :].bitcast(FP8X4), scales=w_scales[:, r, :], in_=w_grp[:, r])
+
+        def x_transpose(b):
+            xw = st[b]["xs"][:].bitcast(F32)
+            st[b]["xt"] = []
+            for cp in range(2):
+                xt = ps_t.tile([P, 2, 256], F32, tag="t", name="xt")
+                for cc in range(2):
+                    c = 2 * cp + cc
+                    for u in range(2):
+                        nc.tensor.transpose(
+                            xt[:, u, P * cc : P * cc + P], xw[:, 256 * c + P * u : 256 * c + P * u + P], ident_f[:]
+                        )
+                st[b]["xt"].append(xt)
+
+        def x_exit(b, cp, on_vector):
+            if cp == 0:
+                st[b]["xg"] = two.tile([P, N * 4], BF16, align_bytes=64, name="xg")
+            dst = st[b]["xg"][:].bitcast(F32).rearrange("p (n u) -> p n u", u=2)[:, 256 * cp : 256 * cp + 256, :]
+            src = st[b]["xt"][cp][:].rearrange("p u n -> p n u")
+            if on_vector:
+                nc.vector.tensor_copy(out=dst, in_=src)
+            else:
+                nc.scalar.copy(out=dst, in_=src)
+
+        def x_quant(b):
+            x_codes = two.tile([P, N], U32, align_bytes=64, name="x_codes")
+            x_scales = two.tile([P, N], U8, align_bytes=64, name="x_scales")
+            nc.vector.quantize_mx(out=x_codes[:].bitcast(FP8X4), scales=x_scales[:], in_=st[b]["xg"][:])
+            st[b]["xc"] = (x_codes, x_scales)
+
+        def mask(b, t0, t1):
+            if t0 == 0:
+                st[b]["lg"] = two.tile([P, NT, N * R], BF16, name="lg")
+            nc.vector.tensor_tensor(
+                out=st[b]["lg"][:, t0:t1, :],
+                in0=st[b]["a"][:, t0:t1, :],
+                in1=st[b]["cap"][:].rearrange("p m r -> p (m r)").unsqueeze(1).to_broadcast([P, t1 - t0, N * R]),
+                op=ALU.min,
+            )
+
+        def row_max(b, t0, t1):
+            if t0 == 0:
+                st[b]["nmx"] = three.tile([P, NT, R], F32, name="nmx")
+            cur = st[b]["lg"][:, t0:t1, :]
+            for width in (512, 256, 128, 64):
+                nxt = one.tile([P, t1 - t0, width], BF16, name="tree%d" % width)
+                nc.vector.tensor_tensor(out=nxt[:], in0=cur[:, :, 0:width], in1=cur[:, :, width : 2 * width], op=ALU.max)
+                cur = nxt[:]
+            mx = three.tile([P, t1 - t0, R], F32, name="mx")
+            nc.vector.tensor_reduce(out=mx[:], in_=cur.rearrange("p t (m r) -> p t r m", r=R), axis=AX.X, op=ALU.max)
+            nc.vector.tensor_scalar(out=st[b]["nmx"][:, t0:t1, :], in0=mx[:], scalar1=-1.0, scalar2=None, op0=ALU.mult)
+
+        def exps(b, t):
+            if t == 0:
+                st[b]["e"] = two.tile([P, NT, R, N], F32, tag="e", name="e", align_bytes=64)
+                st[b]["ssum"] = three.tile([P, NT, R], F32, name="ssum")
+            lg_t = st[b]["lg"][:, t, :].rearrange("p (m r) -> p m r", r=R)
+            for r in range(R):
+                nc.scalar.activation(
+                    out=st[b]["e"][:, t, r, :],
+                    in_=lg_t[:, :, r],
+                    func=ACT.Exp,
+                    bias=st[b]["nmx"][:, t, r : r + 1],
+                    scale=1.0,
+                    accum_out=st[b]["ssum"][:, t, r : r + 1],
+                )
+
+        def recip(b):
+            rs = three.tile([P, NT, R], F32, name="rs")
+            nc.vector.reciprocal(out=rs[:], in_=st[b]["ssum"][:])
+            st[b]["rs"] = rs
+            st[b]["att"] = two.tile([P, R, NT, N], BF16, name="att")
+
+        def norm(b, r):
+            for t in range(NT):
+                nc.vector.tensor_scalar(
+                    out=st[b]["att"][:, r, t, :],
+                    in0=st[b]["e"][:, t, r, :],
+                    scalar1=st[b]["rs"][:, t, r : r + 1],
+                    scalar2=None,
+                    op0=ALU.mult,
+                )
+
+        def a_transpose(b, r, tp):
+            pt = ps_t.tile([P, 2, 4, P], BF16, tag="t", name="pt")
+            for tt in range(2):
+                for j in range(4):
+                    nc.tensor.transpose(pt[:, tt, j, :], st[b]["att"][:, r, 2 * tp + tt, P * j : P * j + P], ident_b[:])
+            st[b]["pt%d%d" % (r, tp)] = pt
+
+        def a_exit(b, r, tp, on_vector):
+            key = "ag%d" % r
+            if key not in st[b]:
+                st[b][key] = two.tile([P, N, 4], BF16, align_bytes=64, name=key)
+            dst = st[b][key][:, 256 * tp : 256 * tp + 256, :].rearrange("p (a n) j -> p a n j", a=2)
+            src = st[b]["pt%d%d" % (r, tp)][:].rearrange("p a j n -> p a n j")
+            if on_vector:
+                nc.vector.tensor_copy(out=dst, in_=src)
+            else:
+                nc.scalar.copy(out=dst, in_=src)
+
+        def a_quant(b, r):
+            codes = two.tile([P, N], U32, align_bytes=64, name="a_codes%d" % r)
+            scales = two.tile([P, N], U8, align_bytes=64, name="a_scales%d" % r)
+            nc.vector.quantize_mx(
+                out=codes[:].bitcast(FP8X4), scales=scales[:], in_=st[b]["ag%d" % r][:].rearrange("p n j -> p (n j)")
+            )
+            st[b]["ac%d" % r] = (codes, scales)
+
+        def h_matmul(b, r, og):
+            ph = ps_h.tile([P, NT, P], F32, name="ph")
+            x_codes, x_scales = st[b]["xc"]
+            for c in range(NT):
+                nc.tensor.matmul_mx(
+                    out=ph[:, c, :],
+                    lhsT=x_codes[:, P * c : P * c + P].bitcast(FP8X4),
+                    lhsT_scale=x_scales[:, P * c : P * c + P],
+                    rhs=w_codes[:, r, P * og : P * og + P].bitcast(FP8X4),
+                    rhs_scale=w_scales[:, r, P * og : P * og + P],
+                    start=True,
+                    stop=True,
+                )
+            st[b]["ph%d%d" % (r, og)] = ph
+
+        def h_exit(b, r, og):
+            key = "hg%d" % r
+            if key not in st[b]:
+                st[b][key] = two.tile([P, H, 4], BF16, align_bytes=64, name=key)
+            nc.scalar.copy(
+                out=st[b][key][:, P * og : P * og + P, :], in_=st[b]["ph%d%d" % (r, og)][:].rearrange("p c o -> p o c")
+            )
+
+        def h_quant(b, r):
+            codes = two.tile([P, H], U32, align_bytes=64, name="h_codes%d" % r)
+            scales = two.tile([P, H], U8, align_bytes=64, name="h_scales%d" % r)
+            nc.vector.quantize_mx(
+                out=codes[:].bitcast(FP8X4), scales=scales[:], in_=st[b]["hg%d" % r][:].rearrange("p o c -> p (o c)")
+            )
+            st[b]["hc%d" % r] = (codes, scales)
+
+        def g_matmul(b, t, r):
+            g = ps_g.tile([P, H], F32, name="g%d" % r)
+            a_codes, a_scales = st[b]["ac%d" % r]
+            h_codes, h_scales = st[b]["hc%d" % r]
+            nc.tensor.matmul_mx(
+                out=g[:],
+                lhsT=a_codes[:, P * t : P * t + P].bitcast(FP8X4),
+                lhsT_scale=a_scales[:, P * t : P * t + P],
+                rhs=h_codes[:].bitcast(FP8X4),
+                rhs_scale=h_scales[:],
+                start=True,
+                stop=True,
+            )
+            st[b]["g%d%d" % (t, r)] = g
+
+        def relu0(b, t):
+            g0 = four.tile([P, H], F32, name="g0s")
+            nc.scalar.activation(out=g0[:], in_=st[b]["g%d0" % t][:], func=ACT.Relu)
+            st[b]["g0s%d" % t] = g0
+
+        def finish(b, t):
+            if t == 0:
+                st[b]["ot"] = two.tile([P, NT, H], F32, name="ot")
+            nc.vector.scalar_tensor_tensor(
+                out=st[b]["ot"][:, t, :],
+                in0=st[b]["g%d1" % t][:],
+                scalar=0.0,
+                in1=st[b]["g0s%d" % t][:],
+                op0=ALU.max,
+                op1=ALU.add,
+            )
+
+        out_v = [out[b].rearrange("(p t) o -> p t o", t=NT) for b in range(B)]
+
+        make_identity(nc, ident_f[:])
+        make_identity(nc, ident_b[:])
+        load_mask(0, N)
+        load_a(0, NT)
+        load_x(0)
+        load_w(0)
+        load_w(1)
+        load_mask(N, B * N)
+        for b in (1, 2):
+            load_a(b, 1)
+            load_x(b)
+        make_cap(0, nc.vector)
+        make_cap(1, nc.gpsimd)
+        make_cap(2, nc.gpsimd)
+        for t in range(NT):
+            mask(0, t, t + 1)
+            row_max(0, t, t + 1)
+            exps(0, t)
+            if t == 1:
+                x_transpose(0)
+                x_exit(0, 0, False)
+                x_exit(0, 1, False)
+        w_group(0)
+        w_quant(0)
+        x_quant(0)
+        w_group(1)
+        w_quant(1)
+        mask(1, 0, NT)
+        row_max(1, 0, NT)
+        for r in range(R):
+            for og in range(4):
+                h_matmul(0, r, og)
+                h_exit(0, r, og)
+        x_transpose(1)
+        x_exit(1, 0, True)
+        x_exit(1, 1, True)
+        x_quant(1)
+        h_quant(0, 0)
+        h_matmul(1, 0, 0)
+        h_matmul(1, 0, 1)
+
+        for i in range(B):
+            last = i == B - 1
+            n1 = i + 1 < B
+            n2 = i + 2 < B
+            pre = i == B - 2
+            if i + 3 < B:
+                load_a(i + 3, 1)
+                load_x(i + 3)
+                make_cap(i + 3, nc.gpsimd)
+            h_quant(i, 1)
+            if last:
+                a_quant(i, 1)
+            if n1:
+                for t in range(NT):
+                    exps(i + 1, t)
+            if not last:
+                recip(i)
+                norm(i, 0)
+                norm(i, 1)
+                a_transpose(i, 0, 0)
+                a_transpose(i, 0, 1)
+                a_exit(i, 0, 0, True)
+                a_exit(i, 0, 1, False)
+                a_transpose(i, 1, 0)
+                a_transpose(i, 1, 1)
+                a_exit(i, 1, 0, False)
+                a_exit(i, 1, 1, False)
+            if n2:
+                mask(i + 2, 0, NT)
+            if pre:
+                recip(i + 1)
+                norm(i + 1, 0)
+            if not last:
+                a_quant(i, 0)
+            if n2:
+                row_max(i + 2, 0, NT)
+            if pre:
+                norm(i + 1, 1)
+            if not last:
+                a_quant(i, 1)
+            if n2:
+                x_transpose(i + 2)
+            g_matmul(i, 0, 0)
+            g_matmul(i, 1, 0)
+            if pre:
+                a_transpose(i + 1, 0, 0)
+                a_transpose(i + 1, 0, 1)
+                a_exit(i + 1, 0, 0, True)
+            if n2:
+                x_exit(i + 2, 0, True)
+                x_exit(i + 2, 1, True)
+                x_quant(i + 2)
+            if n1:
+                h_exit(i + 1, 0, 0)
+                h_exit(i + 1, 0, 1)
+            relu0(i, 0)
+            if n1:
+                h_matmul(i + 1, 0, 2)
+                h_matmul(i + 1, 0, 3)
+                h_exit(i + 1, 0, 2)
+                h_exit(i + 1, 0, 3)
+            if pre:
+                a_transpose(i + 1, 1, 0)
+                a_exit(i + 1, 1, 0, True)
+            relu0(i, 1)
+            g_matmul(i, 2, 0)
+            relu0(i, 2)
+            if n1:
+                h_matmul(i + 1, 1, 0)
+            g_matmul(i, 0, 1)
+            g_matmul(i, 1, 1)
+            if n1:
+                h_exit(i + 1, 1, 0)
+                h_matmul(i + 1, 1, 1)
+            g_matmul(i, 3, 0)
+            relu0(i, 3)
+            if n1:
+                h_exit(i + 1, 1, 1)
+            finish(i, 0)
+            finish(i, 1)
+            if last:
+                nc.sync.dma_start(out=out_v[i][:, 0:2, :], in_=st[i]["ot"][:, 0:2, :])
+            if n1:
+                h_matmul(i + 1, 1, 2)
+            g_matmul(i, 2, 1)
+            g_matmul(i, 3, 1)
+            if n1:
+                h_exit(i + 1, 1, 2)
+            if pre:
+                a_exit(i + 1, 0, 1, False)
+            finish(i, 2)
+            if last:
+                nc.sync.dma_start(out=out_v[i][:, 2:3, :], in_=st[i]["ot"][:, 2:3, :])
+            finish(i, 3)
+            if last:
+                nc.sync.dma_start(out=out_v[i][:, 3:4, :], in_=st[i]["ot"][:, 3:4, :])
+            else:
+                nc.gpsimd.dma_start(out=out_v[i], in_=st[i]["ot"][:])
+            if n1:
+                h_matmul(i + 1, 1, 3)
+                h_exit(i + 1, 1, 3)
+                h_quant(i + 1, 0)
+            if pre:
+                a_transpose(i + 1, 1, 1)
+                a_exit(i + 1, 1, 1, False)
+                a_quant(i + 1, 0)
+            if n2:
+                h_matmul(i + 2, 0, 0)
+                h_matmul(i + 2, 0, 1)

@@ -122,6 +122,7 @@ def tile_rgat_pa_t_kernel(tc, adj, x, dmask, W, out):
         def mask(b, t0, t1):
             if t0 == 0:
                 st[b]["lg"] = two.tile([P, NT, N * R], BF16, name="lg")
+                st[b]["nmx"] = three.tile([P, NT, R], F32, name="nmx")
             nc.vector.tensor_tensor(
                 out=st[b]["lg"][:, t0:t1, :],
                 in0=st[b]["a"][:, t0:t1, :],
@@ -129,17 +130,26 @@ def tile_rgat_pa_t_kernel(tc, adj, x, dmask, W, out):
                 op=ALU.min,
             )
 
-        def row_max(b, t0, t1):
-            if t0 == 0:
-                st[b]["nmx"] = three.tile([P, NT, R], F32, name="nmx")
-            cur = st[b]["lg"][:, t0:t1, :]
-            for width in (512, 256, 128, 64):
-                nxt = one.tile([P, t1 - t0, width], BF16, name="tree%d" % width)
+        def level(b, j, t0, t1):
+            key = "lv%d" % t0
+            if j == 0:
+                cur = st[b]["lg"][:, t0:t1, :]
+            else:
+                cur = st[b][key]
+            if j < 4:
+                width = 512 // (2 ** j)
+                slot = 2 if t1 - t0 == NT else t0 % 2
+                nxt = one.tile([P, t1 - t0, width], BF16, name="tree%d_%d" % (width, slot))
                 nc.vector.tensor_tensor(out=nxt[:], in0=cur[:, :, 0:width], in1=cur[:, :, width : 2 * width], op=ALU.max)
-                cur = nxt[:]
-            mx = three.tile([P, t1 - t0, R], F32, name="mx")
-            nc.vector.tensor_reduce(out=mx[:], in_=cur.rearrange("p t (m r) -> p t r m", r=R), axis=AX.X, op=ALU.max)
-            nc.vector.tensor_scalar(out=st[b]["nmx"][:, t0:t1, :], in0=mx[:], scalar1=-1.0, scalar2=None, op0=ALU.mult)
+                st[b][key] = nxt[:]
+            else:
+                nc.vector.tensor_reduce(
+                    out=st[b]["nmx"][:, t0:t1, :],
+                    in_=cur.rearrange("p t (m r) -> p t r m", r=R),
+                    axis=AX.X,
+                    op=ALU.max,
+                    negate=True,
+                )
 
         def exps(b, t):
             if t == 0:
@@ -277,30 +287,38 @@ def tile_rgat_pa_t_kernel(tc, adj, x, dmask, W, out):
         make_cap(0, nc.vector)
         make_cap(1, nc.gpsimd)
         make_cap(2, nc.gpsimd)
-        for t in range(NT):
+        for t in (0, 2):
             mask(0, t, t + 1)
-            row_max(0, t, t + 1)
+            mask(0, t + 1, t + 2)
+            for j in range(5):
+                level(0, j, t, t + 1)
+                level(0, j, t + 1, t + 2)
             exps(0, t)
-            if t == 1:
+            exps(0, t + 1)
+            if t == 0:
                 x_transpose(0)
                 x_exit(0, 0, False)
                 x_exit(0, 1, False)
         w_group(0)
+        w_group(1)
         w_quant(0)
         x_quant(0)
-        w_group(1)
         w_quant(1)
         mask(1, 0, NT)
-        row_max(1, 0, NT)
         for r in range(R):
             for og in range(4):
                 h_matmul(0, r, og)
                 h_exit(0, r, og)
         x_transpose(1)
+        level(1, 0, 0, NT)
         x_exit(1, 0, True)
+        level(1, 1, 0, NT)
         x_exit(1, 1, True)
-        x_quant(1)
+        level(1, 2, 0, NT)
         h_quant(0, 0)
+        level(1, 3, 0, NT)
+        x_quant(1)
+        level(1, 4, 0, NT)
         h_matmul(1, 0, 0)
         h_matmul(1, 0, 1)
 
@@ -313,6 +331,8 @@ def tile_rgat_pa_t_kernel(tc, adj, x, dmask, W, out):
                 load_a(i + 3, 1)
                 load_x(i + 3)
                 make_cap(i + 3, nc.gpsimd)
+            if not last:
+                recip(i)
             h_quant(i, 1)
             if last:
                 a_quant(i, 1)
@@ -320,7 +340,6 @@ def tile_rgat_pa_t_kernel(tc, adj, x, dmask, W, out):
                 for t in range(NT):
                     exps(i + 1, t)
             if not last:
-                recip(i)
                 norm(i, 0)
                 norm(i, 1)
                 a_transpose(i, 0, 0)
@@ -335,16 +354,17 @@ def tile_rgat_pa_t_kernel(tc, adj, x, dmask, W, out):
                 mask(i + 2, 0, NT)
             if pre:
                 recip(i + 1)
-                norm(i + 1, 0)
             if not last:
                 a_quant(i, 0)
             if n2:
-                row_max(i + 2, 0, NT)
+                level(i + 2, 0, 0, NT)
             if pre:
+                norm(i + 1, 0)
                 norm(i + 1, 1)
             if not last:
                 a_quant(i, 1)
             if n2:
+                level(i + 2, 1, 0, NT)
                 x_transpose(i + 2)
             g_matmul(i, 0, 0)
             g_matmul(i, 1, 0)
@@ -354,8 +374,9 @@ def tile_rgat_pa_t_kernel(tc, adj, x, dmask, W, out):
                 a_exit(i + 1, 0, 0, True)
             if n2:
                 x_exit(i + 2, 0, True)
+                level(i + 2, 2, 0, NT)
                 x_exit(i + 2, 1, True)
-                x_quant(i + 2)
+                level(i + 2, 3, 0, NT)
             if n1:
                 h_exit(i + 1, 0, 0)
                 h_exit(i + 1, 0, 1)
@@ -365,6 +386,10 @@ def tile_rgat_pa_t_kernel(tc, adj, x, dmask, W, out):
                 h_matmul(i + 1, 0, 3)
                 h_exit(i + 1, 0, 2)
                 h_exit(i + 1, 0, 3)
+                h_quant(i + 1, 0)
+            if n2:
+                level(i + 2, 4, 0, NT)
+                x_quant(i + 2)
             if pre:
                 a_transpose(i + 1, 1, 0)
                 a_exit(i + 1, 1, 0, True)
@@ -405,7 +430,6 @@ def tile_rgat_pa_t_kernel(tc, adj, x, dmask, W, out):
             if n1:
                 h_matmul(i + 1, 1, 3)
                 h_exit(i + 1, 1, 3)
-                h_quant(i + 1, 0)
             if pre:
                 a_transpose(i + 1, 1, 1)
                 a_exit(i + 1, 1, 1, False)

@@ -82,9 +82,13 @@ def tile_rgat_pa_t_kernel(tc, adj, x, dmask, W, out):
             st[b]["cap"] = cap
 
         def w_group(r):
-            nc.vector.tensor_copy(
+            nc.gpsimd.tensor_scalar(
                 out=w_grp[:, r].rearrange("p (c i t) -> p c t i", i=4, t=4),
-                in_=w_raw[:, r].rearrange("p (t c i) -> p c t i", t=4, i=4),
+                in0=w_raw[:, r].rearrange("p (t c i) -> p c t i", t=4, i=4),
+                scalar1=1.0,
+                scalar2=0.0,
+                op0=ALU.mult,
+                op1=ALU.add,
             )
 
         def w_quant(r):
@@ -172,15 +176,25 @@ def tile_rgat_pa_t_kernel(tc, adj, x, dmask, W, out):
             st[b]["rs"] = rs
             st[b]["att"] = two.tile([P, R, NT, N], BF16, name="att")
 
-        def norm(b, r):
+        def norm(b, r, on_vector):
             for t in range(NT):
-                nc.vector.tensor_scalar(
-                    out=st[b]["att"][:, r, t, :],
-                    in0=st[b]["e"][:, t, r, :],
-                    scalar1=st[b]["rs"][:, t, r : r + 1],
-                    scalar2=None,
-                    op0=ALU.mult,
-                )
+                if on_vector:
+                    nc.vector.tensor_scalar(
+                        out=st[b]["att"][:, r, t, :],
+                        in0=st[b]["e"][:, t, r, :],
+                        scalar1=st[b]["rs"][:, t, r : r + 1],
+                        scalar2=None,
+                        op0=ALU.mult,
+                    )
+                else:
+                    nc.gpsimd.tensor_scalar(
+                        out=st[b]["att"][:, r, t, :],
+                        in0=st[b]["e"][:, t, r, :],
+                        scalar1=st[b]["rs"][:, t, r : r + 1],
+                        scalar2=0.0,
+                        op0=ALU.mult,
+                        op1=ALU.add,
+                    )
 
         def a_transpose(b, r, tp):
             pt = ps_t.tile([P, 2, 4, P], BF16, tag="t", name="pt")
@@ -273,19 +287,23 @@ def tile_rgat_pa_t_kernel(tc, adj, x, dmask, W, out):
 
         out_v = [out[b].rearrange("(p t) o -> p t o", t=NT) for b in range(B)]
 
+        LAST = B - 1
+
         make_identity(nc, ident_f[:])
-        make_identity(nc, ident_b[:])
         load_mask(0, N)
         load_a(0, NT)
-        load_x(0)
         load_w(0)
         load_w(1)
+        load_x(0)
         load_mask(N, B * N)
         for b in (1, 2):
             load_a(b, 1)
             load_x(b)
         make_cap(0, nc.vector)
         make_cap(1, nc.gpsimd)
+        w_group(0)
+        w_group(1)
+        make_identity(nc, ident_b[:])
         make_cap(2, nc.gpsimd)
         for t in (0, 2):
             mask(0, t, t + 1)
@@ -299,141 +317,168 @@ def tile_rgat_pa_t_kernel(tc, adj, x, dmask, W, out):
                 x_transpose(0)
                 x_exit(0, 0, False)
                 x_exit(0, 1, False)
-        w_group(0)
-        w_group(1)
+        load_a(3, 1)
         w_quant(0)
         x_quant(0)
-        w_quant(1)
         mask(1, 0, NT)
-        for r in range(R):
-            for og in range(4):
-                h_matmul(0, r, og)
-                h_exit(0, r, og)
-        x_transpose(1)
+        w_quant(1)
         level(1, 0, 0, NT)
-        x_exit(1, 0, True)
+        recip(0)
         level(1, 1, 0, NT)
-        x_exit(1, 1, True)
+        norm(0, 0, False)
+        norm(0, 1, False)
+        make_cap(3, nc.gpsimd)
+        h_matmul(0, 0, 0)
+        h_matmul(0, 0, 1)
+        x_transpose(1)
+        h_exit(0, 0, 0)
+        h_exit(0, 0, 1)
+        h_matmul(0, 0, 2)
+        h_matmul(0, 0, 3)
+        x_exit(1, 0, True)
         level(1, 2, 0, NT)
-        h_quant(0, 0)
+        x_exit(1, 1, True)
         level(1, 3, 0, NT)
         x_quant(1)
         level(1, 4, 0, NT)
-        h_matmul(1, 0, 0)
-        h_matmul(1, 0, 1)
+        h_exit(0, 0, 2)
+        h_exit(0, 0, 3)
+        h_matmul(0, 1, 0)
+        h_matmul(0, 1, 1)
+        mask(2, 0, NT)
+        h_quant(0, 0)
+        level(2, 0, 0, NT)
+        a_transpose(0, 0, 0)
+        a_transpose(0, 0, 1)
+        h_exit(0, 1, 0)
+        h_exit(0, 1, 1)
+        h_matmul(0, 1, 2)
+        h_matmul(0, 1, 3)
+        a_exit(0, 0, 0, True)
 
-        for i in range(B):
-            last = i == B - 1
+        for i in range(B + 1):
+            pre = i == LAST - 1
+            fin = i == LAST
+            cur = i < B
             n1 = i + 1 < B
             n2 = i + 2 < B
-            pre = i == B - 2
-            if i + 3 < B:
-                load_a(i + 3, 1)
+            n3 = i + 3 < B
+            if i + 4 < B:
+                load_a(i + 4, 1)
+                make_cap(i + 4, nc.gpsimd)
+            if n3:
                 load_x(i + 3)
-                make_cap(i + 3, nc.gpsimd)
-            if not last:
-                recip(i)
-            h_quant(i, 1)
-            if last:
-                a_quant(i, 1)
             if n1:
-                for t in range(NT):
-                    exps(i + 1, t)
-            if not last:
-                norm(i, 0)
-                norm(i, 1)
-                a_transpose(i, 0, 0)
-                a_transpose(i, 0, 1)
-                a_exit(i, 0, 0, True)
-                a_exit(i, 0, 1, False)
+                exps(i + 1, 0)
+            if i >= 1:
+                finish(i - 1, 2)
+                if i - 1 == LAST:
+                    nc.sync.dma_start(out=out_v[LAST][:, 2:3, :], in_=st[LAST]["ot"][:, 2:3, :])
+                finish(i - 1, 3)
+                if i - 1 == LAST:
+                    nc.sync.dma_start(out=out_v[LAST][:, 3:4, :], in_=st[LAST]["ot"][:, 3:4, :])
+                else:
+                    nc.gpsimd.dma_start(out=out_v[i - 1], in_=st[i - 1]["ot"][:])
+            if cur and not fin:
                 a_transpose(i, 1, 0)
+            if cur:
+                h_exit(i, 1, 2)
+                h_exit(i, 1, 3)
+            if n1:
+                h_matmul(i + 1, 0, 0)
+                h_matmul(i + 1, 0, 1)
+                exps(i + 1, 1)
+                exps(i + 1, 2)
+                exps(i + 1, 3)
+            if cur and not fin:
+                a_exit(i, 0, 1, True)
                 a_transpose(i, 1, 1)
-                a_exit(i, 1, 0, False)
-                a_exit(i, 1, 1, False)
-            if n2:
-                mask(i + 2, 0, NT)
-            if pre:
-                recip(i + 1)
-            if not last:
-                a_quant(i, 0)
-            if n2:
-                level(i + 2, 0, 0, NT)
-            if pre:
-                norm(i + 1, 0)
-                norm(i + 1, 1)
-            if not last:
-                a_quant(i, 1)
             if n2:
                 level(i + 2, 1, 0, NT)
-                x_transpose(i + 2)
-            g_matmul(i, 0, 0)
-            g_matmul(i, 1, 0)
-            if pre:
-                a_transpose(i + 1, 0, 0)
-                a_transpose(i + 1, 0, 1)
-                a_exit(i + 1, 0, 0, True)
+            if cur:
+                h_quant(i, 1)
             if n2:
-                x_exit(i + 2, 0, True)
                 level(i + 2, 2, 0, NT)
-                x_exit(i + 2, 1, True)
+            if cur and not fin:
+                a_quant(i, 0)
+            if n2:
                 level(i + 2, 3, 0, NT)
+            if n1:
+                recip(i + 1)
+            if n2:
+                level(i + 2, 4, 0, NT)
+            if n1:
+                norm(i + 1, 0, i + 1 == LAST)
+                norm(i + 1, 1, i + 1 == LAST)
+            if cur and not fin:
+                g_matmul(i, 0, 0)
+                g_matmul(i, 1, 0)
+                a_exit(i, 1, 0, False)
+            if cur:
+                a_exit(i, 1, 1, False)
+            if n3:
+                mask(i + 3, 0, NT)
+            if cur:
+                a_quant(i, 1)
+            if fin:
+                g_matmul(i, 0, 0)
+                g_matmul(i, 1, 0)
+            if n2:
+                x_transpose(i + 2)
+            if pre:
+                a_transpose(LAST, 0, 0)
+                a_transpose(LAST, 0, 1)
             if n1:
                 h_exit(i + 1, 0, 0)
                 h_exit(i + 1, 0, 1)
-            relu0(i, 0)
-            if n1:
                 h_matmul(i + 1, 0, 2)
                 h_matmul(i + 1, 0, 3)
-                h_exit(i + 1, 0, 2)
-                h_exit(i + 1, 0, 3)
-                h_quant(i + 1, 0)
+            if cur:
+                g_matmul(i, 0, 1)
+                g_matmul(i, 1, 1)
+                relu0(i, 0)
+                relu0(i, 1)
+                g_matmul(i, 2, 0)
+                g_matmul(i, 3, 0)
             if n2:
-                level(i + 2, 4, 0, NT)
+                x_exit(i + 2, 0, True)
+                x_exit(i + 2, 1, True)
+            if n3:
+                level(i + 3, 0, 0, NT)
+            if n2:
                 x_quant(i + 2)
             if pre:
-                a_transpose(i + 1, 1, 0)
-                a_exit(i + 1, 1, 0, True)
-            relu0(i, 1)
-            g_matmul(i, 2, 0)
-            relu0(i, 2)
+                a_exit(LAST, 0, 0, True)
+                a_exit(LAST, 0, 1, True)
+                a_transpose(LAST, 1, 0)
+                a_transpose(LAST, 1, 1)
+                a_quant(LAST, 0)
+            elif n1:
+                a_transpose(i + 1, 0, 0)
+                a_transpose(i + 1, 0, 1)
             if n1:
+                h_exit(i + 1, 0, 2)
+                h_exit(i + 1, 0, 3)
                 h_matmul(i + 1, 1, 0)
-            g_matmul(i, 0, 1)
-            g_matmul(i, 1, 1)
+                h_matmul(i + 1, 1, 1)
+                h_quant(i + 1, 0)
+            if cur:
+                relu0(i, 2)
+                relu0(i, 3)
+                finish(i, 0)
+                finish(i, 1)
+                if fin:
+                    nc.sync.dma_start(out=out_v[LAST][:, 0:2, :], in_=st[LAST]["ot"][:, 0:2, :])
+                g_matmul(i, 2, 1)
             if n1:
                 h_exit(i + 1, 1, 0)
-                h_matmul(i + 1, 1, 1)
-            g_matmul(i, 3, 0)
-            relu0(i, 3)
-            if n1:
                 h_exit(i + 1, 1, 1)
-            finish(i, 0)
-            finish(i, 1)
-            if last:
-                nc.sync.dma_start(out=out_v[i][:, 0:2, :], in_=st[i]["ot"][:, 0:2, :])
-            if n1:
                 h_matmul(i + 1, 1, 2)
-            g_matmul(i, 2, 1)
-            g_matmul(i, 3, 1)
-            if n1:
-                h_exit(i + 1, 1, 2)
-            if pre:
-                a_exit(i + 1, 0, 1, False)
-            finish(i, 2)
-            if last:
-                nc.sync.dma_start(out=out_v[i][:, 2:3, :], in_=st[i]["ot"][:, 2:3, :])
-            finish(i, 3)
-            if last:
-                nc.sync.dma_start(out=out_v[i][:, 3:4, :], in_=st[i]["ot"][:, 3:4, :])
-            else:
-                nc.gpsimd.dma_start(out=out_v[i], in_=st[i]["ot"][:])
+            if cur:
+                g_matmul(i, 3, 1)
             if n1:
                 h_matmul(i + 1, 1, 3)
-                h_exit(i + 1, 1, 3)
             if pre:
-                a_transpose(i + 1, 1, 1)
-                a_exit(i + 1, 1, 1, False)
-                a_quant(i + 1, 0)
-            if n2:
-                h_matmul(i + 2, 0, 0)
-                h_matmul(i + 2, 0, 1)
+                a_exit(LAST, 1, 0, True)
+            elif n1:
+                a_exit(i + 1, 0, 0, True)

@@ -378,7 +378,7 @@ def tile_rgat_pa_t_kernel(tc, adj, x, dmask, W, out):
                 if i - 1 == LAST:
                     nc.sync.dma_start(out=out_v[LAST][:, 3:4, :], in_=st[LAST]["ot"][:, 3:4, :])
                 else:
-                    nc.gpsimd.dma_start(out=out_v[i - 1], in_=st[i - 1]["ot"][:])
+                    nc.sync.dma_start(out=out_v[i - 1], in_=st[i - 1]["ot"][:])
             if cur and not fin:
                 a_transpose(i, 1, 0)
             if cur:

@@ -326,7 +326,7 @@ def tile_rgat_pa_t_kernel(tc, adj, x, dmask, W, out):
         recip(0)
         level(1, 1, 0, NT)
         norm(0, 0, False)
-        norm(0, 1, False)
+        norm(0, 1, True)
         make_cap(3, nc.gpsimd)
         h_matmul(0, 0, 0)
         h_matmul(0, 0, 1)
@@ -409,7 +409,7 @@ def tile_rgat_pa_t_kernel(tc, adj, x, dmask, W, out):
                 level(i + 2, 4, 0, NT)
             if n1:
                 norm(i + 1, 0, i + 1 == LAST)
-                norm(i + 1, 1, i + 1 == LAST)
+                norm(i + 1, 1, True)
             if cur and not fin:
                 g_matmul(i, 0, 0)
                 g_matmul(i, 1, 0)

@@ -30,14 +30,15 @@ def tile_rgat_pa_t_kernel(tc, adj, x, dmask, W, out):
         two = ctx.enter_context(tc.tile_pool(name="two", bufs=2))
         three = ctx.enter_context(tc.tile_pool(name="three", bufs=3))
         four = ctx.enter_context(tc.tile_pool(name="four", bufs=4))
-        ps_t = ctx.enter_context(tc.psum_pool(name="ps_t", bufs=2))
+        ps_e = ctx.enter_context(tc.psum_pool(name="ps_e", bufs=2))
+        ps_x = ctx.enter_context(tc.psum_pool(name="ps_x", bufs=2))
         ps_h = ctx.enter_context(tc.psum_pool(name="ps_h", bufs=2))
-        ps_g = ctx.enter_context(tc.psum_pool(name="ps_g", bufs=2))
+        ps_g = ctx.enter_context(tc.psum_pool(name="ps_g", bufs=1))
 
         st = [dict() for b in range(B)]
+        LAST = B - 1
 
         ident_f = const.tile([P, P], F32)
-        ident_b = const.tile([P, P], BF16)
         dm = const.tile([P, B * N], BF16)
         w_codes = const.tile([P, R, H], U32, align_bytes=64)
         w_scales = const.tile([P, R, H], U8, align_bytes=64)
@@ -45,6 +46,7 @@ def tile_rgat_pa_t_kernel(tc, adj, x, dmask, W, out):
         w_raw = w_stage[:, 0]
         w_grp = w_stage[:, 1]
         dm_row = dmask.rearrange("b o m -> (b o m)")
+        out_v = [out[b].rearrange("(p t) o -> p t o", t=NT) for b in range(B)]
 
         def load_mask(lo, hi):
             nc.scalar.dma_start(out=dm[:, lo:hi], in_=dm_row[lo:hi].partition_broadcast(P))
@@ -94,28 +96,22 @@ def tile_rgat_pa_t_kernel(tc, adj, x, dmask, W, out):
         def w_quant(r):
             nc.vector.quantize_mx(out=w_codes[:, r, :].bitcast(FP8X4), scales=w_scales[:, r, :], in_=w_grp[:, r])
 
-        def x_transpose(b):
+        def x_transpose(b, cp):
             xw = st[b]["xs"][:].bitcast(F32)
-            st[b]["xt"] = []
-            for cp in range(2):
-                xt = ps_t.tile([P, 2, 256], F32, tag="t", name="xt")
-                for cc in range(2):
-                    c = 2 * cp + cc
-                    for u in range(2):
-                        nc.tensor.transpose(
-                            xt[:, u, P * cc : P * cc + P], xw[:, 256 * c + P * u : 256 * c + P * u + P], ident_f[:]
-                        )
-                st[b]["xt"].append(xt)
+            xt = ps_x.tile([P, 2, 256], F32, name="xt")
+            for cc in range(2):
+                c = 2 * cp + cc
+                for u in range(2):
+                    nc.tensor.transpose(
+                        xt[:, u, P * cc : P * cc + P], xw[:, 256 * c + P * u : 256 * c + P * u + P], ident_f[:]
+                    )
+            st[b]["xt%d" % cp] = xt
 
-        def x_exit(b, cp, on_vector):
+        def x_exit(b, cp):
             if cp == 0:
                 st[b]["xg"] = two.tile([P, N * 4], BF16, align_bytes=64, name="xg")
             dst = st[b]["xg"][:].bitcast(F32).rearrange("p (n u) -> p n u", u=2)[:, 256 * cp : 256 * cp + 256, :]
-            src = st[b]["xt"][cp][:].rearrange("p u n -> p n u")
-            if on_vector:
-                nc.vector.tensor_copy(out=dst, in_=src)
-            else:
-                nc.scalar.copy(out=dst, in_=src)
+            nc.scalar.copy(out=dst, in_=st[b]["xt%d" % cp][:].rearrange("p u n -> p n u"))
 
         def x_quant(b):
             x_codes = two.tile([P, N], U32, align_bytes=64, name="x_codes")
@@ -155,40 +151,29 @@ def tile_rgat_pa_t_kernel(tc, adj, x, dmask, W, out):
                     negate=True,
                 )
 
-        def exps(b, t):
-            if t == 0:
+        def exp1(b, t, r):
+            if t == 0 and r == 0:
                 st[b]["e"] = two.tile([P, NT, R, N], F32, tag="e", name="e", align_bytes=64)
                 st[b]["ssum"] = three.tile([P, NT, R], F32, name="ssum")
-            lg_t = st[b]["lg"][:, t, :].rearrange("p (m r) -> p m r", r=R)
-            for r in range(R):
-                nc.scalar.activation(
-                    out=st[b]["e"][:, t, r, :],
-                    in_=lg_t[:, :, r],
-                    func=ACT.Exp,
-                    bias=st[b]["nmx"][:, t, r : r + 1],
-                    scale=1.0,
-                    accum_out=st[b]["ssum"][:, t, r : r + 1],
-                )
+            nc.scalar.activation(
+                out=st[b]["e"][:, t, r, :],
+                in_=st[b]["lg"][:, t, :].rearrange("p (m r) -> p m r", r=R)[:, :, r],
+                func=ACT.Exp,
+                bias=st[b]["nmx"][:, t, r : r + 1],
+                scale=1.0,
+                accum_out=st[b]["ssum"][:, t, r : r + 1],
+            )
 
         def recip(b):
             rs = three.tile([P, NT, R], F32, name="rs")
             nc.vector.reciprocal(out=rs[:], in_=st[b]["ssum"][:])
             st[b]["rs"] = rs
-            st[b]["att"] = two.tile([P, R, NT, N], BF16, name="att")
 
-        def norm(b, r, on_vector):
-            for t in range(NT):
-                if on_vector:
-                    nc.vector.tensor_scalar(
-                        out=st[b]["att"][:, r, t, :],
-                        in0=st[b]["e"][:, t, r, :],
-                        scalar1=st[b]["rs"][:, t, r : r + 1],
-                        scalar2=None,
-                        op0=ALU.mult,
-                    )
-                else:
+        def norm(b):
+            for r in range(R):
+                for t in range(NT):
                     nc.gpsimd.tensor_scalar(
-                        out=st[b]["att"][:, r, t, :],
+                        out=st[b]["e"][:, t, r, :],
                         in0=st[b]["e"][:, t, r, :],
                         scalar1=st[b]["rs"][:, t, r : r + 1],
                         scalar2=0.0,
@@ -196,19 +181,18 @@ def tile_rgat_pa_t_kernel(tc, adj, x, dmask, W, out):
                         op1=ALU.add,
                     )
 
-        def a_transpose(b, r, tp):
-            pt = ps_t.tile([P, 2, 4, P], BF16, tag="t", name="pt")
-            for tt in range(2):
-                for j in range(4):
-                    nc.tensor.transpose(pt[:, tt, j, :], st[b]["att"][:, r, 2 * tp + tt, P * j : P * j + P], ident_b[:])
-            st[b]["pt%d%d" % (r, tp)] = pt
+        def a_transpose(b, r, t):
+            pt = ps_e.tile([P, 4, P], F32, name="pt")
+            for j in range(4):
+                nc.tensor.transpose(pt[:, j, :], st[b]["e"][:, t, r, P * j : P * j + P], ident_f[:])
+            st[b]["pt%d%d" % (r, t)] = pt
 
-        def a_exit(b, r, tp, on_vector):
+        def a_exit(b, r, t, on_vector):
             key = "ag%d" % r
             if key not in st[b]:
                 st[b][key] = two.tile([P, N, 4], BF16, align_bytes=64, name=key)
-            dst = st[b][key][:, 256 * tp : 256 * tp + 256, :].rearrange("p (a n) j -> p a n j", a=2)
-            src = st[b]["pt%d%d" % (r, tp)][:].rearrange("p a j n -> p a n j")
+            dst = st[b][key][:, P * t : P * t + P, :]
+            src = st[b]["pt%d%d" % (r, t)][:].rearrange("p j n -> p n j")
             if on_vector:
                 nc.vector.tensor_copy(out=dst, in_=src)
             else:
@@ -284,10 +268,10 @@ def tile_rgat_pa_t_kernel(tc, adj, x, dmask, W, out):
                 op0=ALU.max,
                 op1=ALU.add,
             )
-
-        out_v = [out[b].rearrange("(p t) o -> p t o", t=NT) for b in range(B)]
-
-        LAST = B - 1
+            if b == LAST:
+                nc.sync.dma_start(out=out_v[b][:, t : t + 1, :], in_=st[b]["ot"][:, t : t + 1, :])
+            elif t == NT - 1:
+                nc.sync.dma_start(out=out_v[b], in_=st[b]["ot"][:])
 
         make_identity(nc, ident_f[:])
         load_mask(0, N)
@@ -303,7 +287,6 @@ def tile_rgat_pa_t_kernel(tc, adj, x, dmask, W, out):
         make_cap(1, nc.gpsimd)
         w_group(0)
         w_group(1)
-        make_identity(nc, ident_b[:])
         make_cap(2, nc.gpsimd)
         for t in (0, 2):
             mask(0, t, t + 1)
@@ -311,174 +294,157 @@ def tile_rgat_pa_t_kernel(tc, adj, x, dmask, W, out):
             for j in range(5):
                 level(0, j, t, t + 1)
                 level(0, j, t + 1, t + 2)
-            exps(0, t)
-            exps(0, t + 1)
+            for tt in (t, t + 1):
+                exp1(0, tt, 0)
+                exp1(0, tt, 1)
             if t == 0:
-                x_transpose(0)
-                x_exit(0, 0, False)
-                x_exit(0, 1, False)
+                x_transpose(0, 0)
+                x_transpose(0, 1)
+                x_exit(0, 0)
+                x_exit(0, 1)
         load_a(3, 1)
+        make_cap(3, nc.gpsimd)
         w_quant(0)
         x_quant(0)
         mask(1, 0, NT)
         w_quant(1)
         level(1, 0, 0, NT)
-        recip(0)
-        level(1, 1, 0, NT)
-        norm(0, 0, False)
-        norm(0, 1, True)
-        make_cap(3, nc.gpsimd)
+        x_transpose(1, 0)
+        x_transpose(1, 1)
         h_matmul(0, 0, 0)
         h_matmul(0, 0, 1)
-        x_transpose(1)
-        h_exit(0, 0, 0)
-        h_exit(0, 0, 1)
-        h_matmul(0, 0, 2)
-        h_matmul(0, 0, 3)
-        x_exit(1, 0, True)
+        level(1, 1, 0, NT)
         level(1, 2, 0, NT)
-        x_exit(1, 1, True)
         level(1, 3, 0, NT)
-        x_quant(1)
-        level(1, 4, 0, NT)
-        h_exit(0, 0, 2)
-        h_exit(0, 0, 3)
-        h_matmul(0, 1, 0)
-        h_matmul(0, 1, 1)
-        mask(2, 0, NT)
-        h_quant(0, 0)
-        level(2, 0, 0, NT)
-        a_transpose(0, 0, 0)
-        a_transpose(0, 0, 1)
-        h_exit(0, 1, 0)
-        h_exit(0, 1, 1)
-        h_matmul(0, 1, 2)
-        h_matmul(0, 1, 3)
-        a_exit(0, 0, 0, True)
 
-        for i in range(B + 1):
-            pre = i == LAST - 1
-            fin = i == LAST
-            cur = i < B
-            n1 = i + 1 < B
-            n2 = i + 2 < B
-            n3 = i + 3 < B
-            if i + 4 < B:
+        for i in range(-1, B + 1):
+            c0 = 0 <= i < B
+            c1 = i + 1 < B
+            c2 = i + 2 < B
+            c3 = i + 3 < B
+            if 0 <= i and i + 4 < B:
                 load_a(i + 4, 1)
                 make_cap(i + 4, nc.gpsimd)
-            if n3:
-                load_x(i + 3)
-            if n1:
-                exps(i + 1, 0)
-            if i >= 1:
-                finish(i - 1, 2)
-                if i - 1 == LAST:
-                    nc.sync.dma_start(out=out_v[LAST][:, 2:3, :], in_=st[LAST]["ot"][:, 2:3, :])
-                finish(i - 1, 3)
-                if i - 1 == LAST:
-                    nc.sync.dma_start(out=out_v[LAST][:, 3:4, :], in_=st[LAST]["ot"][:, 3:4, :])
-                else:
-                    nc.sync.dma_start(out=out_v[i - 1], in_=st[i - 1]["ot"][:])
-            if cur and not fin:
-                a_transpose(i, 1, 0)
-            if cur:
-                h_exit(i, 1, 2)
-                h_exit(i, 1, 3)
-            if n1:
-                h_matmul(i + 1, 0, 0)
-                h_matmul(i + 1, 0, 1)
-                exps(i + 1, 1)
-                exps(i + 1, 2)
-                exps(i + 1, 3)
-            if cur and not fin:
-                a_exit(i, 0, 1, True)
-                a_transpose(i, 1, 1)
-            if n2:
-                level(i + 2, 1, 0, NT)
-            if cur:
-                h_quant(i, 1)
-            if n2:
-                level(i + 2, 2, 0, NT)
-            if cur and not fin:
-                a_quant(i, 0)
-            if n2:
-                level(i + 2, 3, 0, NT)
-            if n1:
+                load_x(i + 4)
+            if i == -1:
+                load_x(3)
+            if c2:
+                x_exit(i + 2, 0)
+                x_exit(i + 2, 1)
+            if c1:
                 recip(i + 1)
-            if n2:
+            if c2:
                 level(i + 2, 4, 0, NT)
-            if n1:
-                norm(i + 1, 0, i + 1 == LAST)
-                norm(i + 1, 1, True)
-            if cur and not fin:
-                g_matmul(i, 0, 0)
-                g_matmul(i, 1, 0)
-                a_exit(i, 1, 0, False)
-            if cur:
-                a_exit(i, 1, 1, False)
-            if n3:
-                mask(i + 3, 0, NT)
-            if cur:
-                a_quant(i, 1)
-            if fin:
-                g_matmul(i, 0, 0)
-                g_matmul(i, 1, 0)
-            if n2:
-                x_transpose(i + 2)
-            if pre:
-                a_transpose(LAST, 0, 0)
-                a_transpose(LAST, 0, 1)
-            if n1:
+            if c1:
+                norm(i + 1)
+            if c0:
+                a_transpose(i, 1, 3)
+            if c3:
+                x_transpose(i + 3, 0)
+                x_transpose(i + 3, 1)
+            if c1:
                 h_exit(i + 1, 0, 0)
+            if c0:
+                a_exit(i, 1, 3, False)
+            if c1:
                 h_exit(i + 1, 0, 1)
+            if c0:
+                a_quant(i, 1)
+            if c1:
                 h_matmul(i + 1, 0, 2)
                 h_matmul(i + 1, 0, 3)
-            if cur:
-                g_matmul(i, 0, 1)
-                g_matmul(i, 1, 1)
-                relu0(i, 0)
-                relu0(i, 1)
-                g_matmul(i, 2, 0)
-                g_matmul(i, 3, 0)
-            if n2:
-                x_exit(i + 2, 0, True)
-                x_exit(i + 2, 1, True)
-            if n3:
-                level(i + 3, 0, 0, NT)
-            if n2:
+            if c3:
+                mask(i + 3, 0, NT)
+            if c2:
                 x_quant(i + 2)
-            if pre:
-                a_exit(LAST, 0, 0, True)
-                a_exit(LAST, 0, 1, True)
-                a_transpose(LAST, 1, 0)
-                a_transpose(LAST, 1, 1)
-                a_quant(LAST, 0)
-            elif n1:
+            if c1:
                 a_transpose(i + 1, 0, 0)
+            if c0:
+                g_matmul(i, 0, 1)
+            if c1:
                 a_transpose(i + 1, 0, 1)
-            if n1:
+            if c0:
+                relu0(i, 0)
+                g_matmul(i, 1, 0)
+            if c1:
                 h_exit(i + 1, 0, 2)
                 h_exit(i + 1, 0, 3)
+            if c2:
+                exp1(i + 2, 0, 0)
+            if c1:
                 h_matmul(i + 1, 1, 0)
                 h_matmul(i + 1, 1, 1)
-                h_quant(i + 1, 0)
-            if cur:
-                relu0(i, 2)
-                relu0(i, 3)
+                a_exit(i + 1, 0, 0, True)
+            if c3:
+                level(i + 3, 0, 0, NT)
+            if c1:
+                a_exit(i + 1, 0, 1, True)
+            if c0:
                 finish(i, 0)
-                finish(i, 1)
-                if fin:
-                    nc.sync.dma_start(out=out_v[LAST][:, 0:2, :], in_=st[LAST]["ot"][:, 0:2, :])
-                g_matmul(i, 2, 1)
-            if n1:
+            if c1:
+                h_quant(i + 1, 0)
+            if c0:
+                relu0(i, 1)
+            if c1:
                 h_exit(i + 1, 1, 0)
                 h_exit(i + 1, 1, 1)
+            if c0:
+                g_matmul(i, 2, 0)
+            if c1:
                 h_matmul(i + 1, 1, 2)
-            if cur:
-                g_matmul(i, 3, 1)
-            if n1:
+                a_transpose(i + 1, 0, 2)
                 h_matmul(i + 1, 1, 3)
-            if pre:
-                a_exit(LAST, 1, 0, True)
-            elif n1:
-                a_exit(i + 1, 0, 0, True)
+            if c0:
+                relu0(i, 2)
+            if c2:
+                exp1(i + 2, 0, 1)
+            if c1:
+                h_exit(i + 1, 1, 2)
+                h_exit(i + 1, 1, 3)
+            if c0:
+                g_matmul(i, 3, 0)
+            if c1:
+                a_transpose(i + 1, 0, 3)
+            if c0:
+                g_matmul(i, 1, 1)
+            if c2:
+                h_matmul(i + 2, 0, 0)
+                h_matmul(i + 2, 0, 1)
+            if c1:
+                a_exit(i + 1, 0, 2, True)
+            if c0:
+                finish(i, 1)
+            if c1:
+                a_exit(i + 1, 0, 3, True)
+                a_transpose(i + 1, 1, 0)
+            if c0:
+                g_matmul(i, 2, 1)
+            if c1:
+                a_transpose(i + 1, 1, 1)
+                a_exit(i + 1, 1, 0, True)
+                a_quant(i + 1, 0)
+            if c0:
+                finish(i, 2)
+            if c3:
+                level(i + 3, 1, 0, NT)
+            if c1:
+                a_exit(i + 1, 1, 1, True)
+                h_quant(i + 1, 1)
+            if c0:
+                relu0(i, 3)
+            if c2:
+                for t in (1, 2, 3):
+                    exp1(i + 2, t, 0)
+                    exp1(i + 2, t, 1)
+            if c1:
+                a_transpose(i + 1, 1, 2)
+                g_matmul(i + 1, 0, 0)
+            if c0:
+                g_matmul(i, 3, 1)
+                finish(i, 3)
+            if c3:
+                level(i + 3, 2, 0, NT)
+            if c1:
+                a_exit(i + 1, 1, 2, True)
+            if c3:
+                level(i + 3, 3, 0, NT)

@@ -30,15 +30,12 @@ def tile_rgat_pa_t_kernel(tc, adj, x, dmask, W, out):
         two = ctx.enter_context(tc.tile_pool(name="two", bufs=2))
         three = ctx.enter_context(tc.tile_pool(name="three", bufs=3))
         four = ctx.enter_context(tc.tile_pool(name="four", bufs=4))
-        ps_e = ctx.enter_context(tc.psum_pool(name="ps_e", bufs=2))
-        ps_x = ctx.enter_context(tc.psum_pool(name="ps_x", bufs=2))
-        ps_h = ctx.enter_context(tc.psum_pool(name="ps_h", bufs=2))
-        ps_g = ctx.enter_context(tc.psum_pool(name="ps_g", bufs=1))
+        banks = ctx.enter_context(tc.psum_pool(name="banks", bufs=8))
 
         st = [dict() for b in range(B)]
-        LAST = B - 1
 
         ident_f = const.tile([P, P], F32)
+        ident_b = const.tile([P, P], BF16)
         dm = const.tile([P, B * N], BF16)
         w_codes = const.tile([P, R, H], U32, align_bytes=64)
         w_scales = const.tile([P, R, H], U8, align_bytes=64)
@@ -46,7 +43,6 @@ def tile_rgat_pa_t_kernel(tc, adj, x, dmask, W, out):
         w_raw = w_stage[:, 0]
         w_grp = w_stage[:, 1]
         dm_row = dmask.rearrange("b o m -> (b o m)")
-        out_v = [out[b].rearrange("(p t) o -> p t o", t=NT) for b in range(B)]
 
         def load_mask(lo, hi):
             nc.scalar.dma_start(out=dm[:, lo:hi], in_=dm_row[lo:hi].partition_broadcast(P))
@@ -96,22 +92,28 @@ def tile_rgat_pa_t_kernel(tc, adj, x, dmask, W, out):
         def w_quant(r):
             nc.vector.quantize_mx(out=w_codes[:, r, :].bitcast(FP8X4), scales=w_scales[:, r, :], in_=w_grp[:, r])
 
-        def x_transpose(b, cp):
+        def x_transpose(b):
             xw = st[b]["xs"][:].bitcast(F32)
-            xt = ps_x.tile([P, 2, 256], F32, name="xt")
-            for cc in range(2):
-                c = 2 * cp + cc
-                for u in range(2):
-                    nc.tensor.transpose(
-                        xt[:, u, P * cc : P * cc + P], xw[:, 256 * c + P * u : 256 * c + P * u + P], ident_f[:]
-                    )
-            st[b]["xt%d" % cp] = xt
+            st[b]["xt"] = []
+            for cp in range(2):
+                xt = banks.tile([P, 2, 256], F32, tag="bank", name="xt")
+                for cc in range(2):
+                    c = 2 * cp + cc
+                    for u in range(2):
+                        nc.tensor.transpose(
+                            xt[:, u, P * cc : P * cc + P], xw[:, 256 * c + P * u : 256 * c + P * u + P], ident_f[:]
+                        )
+                st[b]["xt"].append(xt)
 
-        def x_exit(b, cp):
+        def x_exit(b, cp, on_vector):
             if cp == 0:
                 st[b]["xg"] = two.tile([P, N * 4], BF16, align_bytes=64, name="xg")
             dst = st[b]["xg"][:].bitcast(F32).rearrange("p (n u) -> p n u", u=2)[:, 256 * cp : 256 * cp + 256, :]
-            nc.scalar.copy(out=dst, in_=st[b]["xt%d" % cp][:].rearrange("p u n -> p n u"))
+            src = st[b]["xt"][cp][:].rearrange("p u n -> p n u")
+            if on_vector:
+                nc.vector.tensor_copy(out=dst, in_=src)
+            else:
+                nc.scalar.copy(out=dst, in_=src)
 
         def x_quant(b):
             x_codes = two.tile([P, N], U32, align_bytes=64, name="x_codes")
@@ -151,29 +153,40 @@ def tile_rgat_pa_t_kernel(tc, adj, x, dmask, W, out):
                     negate=True,
                 )
 
-        def exp1(b, t, r):
-            if t == 0 and r == 0:
+        def exps(b, t):
+            if t == 0:
                 st[b]["e"] = two.tile([P, NT, R, N], F32, tag="e", name="e", align_bytes=64)
                 st[b]["ssum"] = three.tile([P, NT, R], F32, name="ssum")
-            nc.scalar.activation(
-                out=st[b]["e"][:, t, r, :],
-                in_=st[b]["lg"][:, t, :].rearrange("p (m r) -> p m r", r=R)[:, :, r],
-                func=ACT.Exp,
-                bias=st[b]["nmx"][:, t, r : r + 1],
-                scale=1.0,
-                accum_out=st[b]["ssum"][:, t, r : r + 1],
-            )
+            lg_t = st[b]["lg"][:, t, :].rearrange("p (m r) -> p m r", r=R)
+            for r in range(R):
+                nc.scalar.activation(
+                    out=st[b]["e"][:, t, r, :],
+                    in_=lg_t[:, :, r],
+                    func=ACT.Exp,
+                    bias=st[b]["nmx"][:, t, r : r + 1],
+                    scale=1.0,
+                    accum_out=st[b]["ssum"][:, t, r : r + 1],
+                )
 
         def recip(b):
             rs = three.tile([P, NT, R], F32, name="rs")
             nc.vector.reciprocal(out=rs[:], in_=st[b]["ssum"][:])
             st[b]["rs"] = rs
+            st[b]["att"] = two.tile([P, R, NT, N], BF16, name="att")
 
-        def norm(b):
-            for r in range(R):
-                for t in range(NT):
+        def norm(b, r, on_vector):
+            for t in range(NT):
+                if on_vector:
+                    nc.vector.tensor_scalar(
+                        out=st[b]["att"][:, r, t, :],
+                        in0=st[b]["e"][:, t, r, :],
+                        scalar1=st[b]["rs"][:, t, r : r + 1],
+                        scalar2=None,
+                        op0=ALU.mult,
+                    )
+                else:
                     nc.gpsimd.tensor_scalar(
-                        out=st[b]["e"][:, t, r, :],
+                        out=st[b]["att"][:, r, t, :],
                         in0=st[b]["e"][:, t, r, :],
                         scalar1=st[b]["rs"][:, t, r : r + 1],
                         scalar2=0.0,
@@ -181,18 +194,19 @@ def tile_rgat_pa_t_kernel(tc, adj, x, dmask, W, out):
                         op1=ALU.add,
                     )
 
-        def a_transpose(b, r, t):
-            pt = ps_e.tile([P, 4, P], F32, name="pt")
-            for j in range(4):
-                nc.tensor.transpose(pt[:, j, :], st[b]["e"][:, t, r, P * j : P * j + P], ident_f[:])
-            st[b]["pt%d%d" % (r, t)] = pt
+        def a_transpose(b, r, tp):
+            pt = banks.tile([P, 2, 4, P], BF16, tag="bank", name="pt")
+            for tt in range(2):
+                for j in range(4):
+                    nc.tensor.transpose(pt[:, tt, j, :], st[b]["att"][:, r, 2 * tp + tt, P * j : P * j + P], ident_b[:])
+            st[b]["pt%d%d" % (r, tp)] = pt
 
-        def a_exit(b, r, t, on_vector):
+        def a_exit(b, r, tp, on_vector):
             key = "ag%d" % r
             if key not in st[b]:
                 st[b][key] = two.tile([P, N, 4], BF16, align_bytes=64, name=key)
-            dst = st[b][key][:, P * t : P * t + P, :]
-            src = st[b]["pt%d%d" % (r, t)][:].rearrange("p j n -> p n j")
+            dst = st[b][key][:, 256 * tp : 256 * tp + 256, :].rearrange("p (a n) j -> p a n j", a=2)
+            src = st[b]["pt%d%d" % (r, tp)][:].rearrange("p a j n -> p a n j")
             if on_vector:
                 nc.vector.tensor_copy(out=dst, in_=src)
             else:
@@ -207,7 +221,7 @@ def tile_rgat_pa_t_kernel(tc, adj, x, dmask, W, out):
             st[b]["ac%d" % r] = (codes, scales)
 
         def h_matmul(b, r, og):
-            ph = ps_h.tile([P, NT, P], F32, name="ph")
+            ph = banks.tile([P, NT, P], F32, tag="bank", name="ph")
             x_codes, x_scales = st[b]["xc"]
             for c in range(NT):
                 nc.tensor.matmul_mx(
@@ -238,7 +252,7 @@ def tile_rgat_pa_t_kernel(tc, adj, x, dmask, W, out):
             st[b]["hc%d" % r] = (codes, scales)
 
         def g_matmul(b, t, r):
-            g = ps_g.tile([P, H], F32, name="g%d" % r)
+            g = banks.tile([P, H], F32, tag="bank", name="g%d" % r)
             a_codes, a_scales = st[b]["ac%d" % r]
             h_codes, h_scales = st[b]["hc%d" % r]
             nc.tensor.matmul_mx(
@@ -268,10 +282,13 @@ def tile_rgat_pa_t_kernel(tc, adj, x, dmask, W, out):
                 op0=ALU.max,
                 op1=ALU.add,
             )
-            if b == LAST:
-                nc.sync.dma_start(out=out_v[b][:, t : t + 1, :], in_=st[b]["ot"][:, t : t + 1, :])
-            elif t == NT - 1:
-                nc.sync.dma_start(out=out_v[b], in_=st[b]["ot"][:])
+
+        out_v = [out[b].rearrange("(p t) o -> p t o", t=NT) for b in range(B)]
+
+        LAST = B - 1
+
+        def store(b, t0, t1):
+            nc.sync.dma_start(out=out_v[b][:, t0:t1, :], in_=st[b]["ot"][:, t0:t1, :])
 
         make_identity(nc, ident_f[:])
         load_mask(0, N)
@@ -287,6 +304,7 @@ def tile_rgat_pa_t_kernel(tc, adj, x, dmask, W, out):
         make_cap(1, nc.gpsimd)
         w_group(0)
         w_group(1)
+        make_identity(nc, ident_b[:])
         make_cap(2, nc.gpsimd)
         for t in (0, 2):
             mask(0, t, t + 1)
@@ -294,157 +312,115 @@ def tile_rgat_pa_t_kernel(tc, adj, x, dmask, W, out):
             for j in range(5):
                 level(0, j, t, t + 1)
                 level(0, j, t + 1, t + 2)
-            for tt in (t, t + 1):
-                exp1(0, tt, 0)
-                exp1(0, tt, 1)
+            exps(0, t)
+            exps(0, t + 1)
             if t == 0:
-                x_transpose(0, 0)
-                x_transpose(0, 1)
-                x_exit(0, 0)
-                x_exit(0, 1)
+                x_transpose(0)
+                x_exit(0, 0, False)
+                x_exit(0, 1, False)
         load_a(3, 1)
         make_cap(3, nc.gpsimd)
         w_quant(0)
         x_quant(0)
+        recip(0)
         mask(1, 0, NT)
         w_quant(1)
+        norm(0, 0, False)
+        norm(0, 1, False)
+        x_transpose(1)
+        for k in range(8):
+            h_matmul(0, k // 4, k % 4)
         level(1, 0, 0, NT)
-        x_transpose(1, 0)
-        x_transpose(1, 1)
-        h_matmul(0, 0, 0)
-        h_matmul(0, 0, 1)
+        x_exit(1, 0, True)
         level(1, 1, 0, NT)
+        x_exit(1, 1, True)
         level(1, 2, 0, NT)
+        x_quant(1)
         level(1, 3, 0, NT)
+        level(1, 4, 0, NT)
+        for k in range(8):
+            h_exit(0, k // 4, k % 4)
+        mask(2, 0, NT)
+        h_quant(0, 0)
+        level(2, 0, 0, NT)
+        h_quant(0, 1)
 
-        for i in range(-1, B + 1):
-            c0 = 0 <= i < B
-            c1 = i + 1 < B
-            c2 = i + 2 < B
-            c3 = i + 3 < B
-            if 0 <= i and i + 4 < B:
+        for i in range(B):
+            pre = i == LAST - 1
+            fin = i == LAST
+            n1 = i + 1 < B
+            n2 = i + 2 < B
+            n3 = i + 3 < B
+            if i + 4 < B:
                 load_a(i + 4, 1)
                 make_cap(i + 4, nc.gpsimd)
-                load_x(i + 4)
-            if i == -1:
-                load_x(3)
-            if c2:
-                x_exit(i + 2, 0)
-                x_exit(i + 2, 1)
-            if c1:
-                recip(i + 1)
-            if c2:
+            if n3:
+                load_x(i + 3)
+            if not fin:
+                for k in range(4):
+                    a_transpose(i, k // 2, k % 2)
+            if n2:
+                x_transpose(i + 2)
+            if n1:
+                for t in range(NT):
+                    exps(i + 1, t)
+            if not fin:
+                a_exit(i, 0, 0, True)
+                if n2:
+                    level(i + 2, 1, 0, NT)
+                a_exit(i, 0, 1, True)
+                if n2:
+                    level(i + 2, 2, 0, NT)
+                a_quant(i, 0)
+                if n2:
+                    level(i + 2, 3, 0, NT)
+            if n2:
+                x_exit(i + 2, 0, True)
                 level(i + 2, 4, 0, NT)
-            if c1:
-                norm(i + 1)
-            if c0:
-                a_transpose(i, 1, 3)
-            if c3:
-                x_transpose(i + 3, 0)
-                x_transpose(i + 3, 1)
-            if c1:
-                h_exit(i + 1, 0, 0)
-            if c0:
-                a_exit(i, 1, 3, False)
-            if c1:
-                h_exit(i + 1, 0, 1)
-            if c0:
-                a_quant(i, 1)
-            if c1:
-                h_matmul(i + 1, 0, 2)
-                h_matmul(i + 1, 0, 3)
-            if c3:
-                mask(i + 3, 0, NT)
-            if c2:
+                x_exit(i + 2, 1, True)
+            if n1:
+                recip(i + 1)
+                norm(i + 1, 0, i + 1 == LAST)
+                norm(i + 1, 1, i + 1 == LAST)
+            if not fin:
+                a_exit(i, 1, 0, False)
+                a_exit(i, 1, 1, False)
+            if n2:
                 x_quant(i + 2)
-            if c1:
-                a_transpose(i + 1, 0, 0)
-            if c0:
-                g_matmul(i, 0, 1)
-            if c1:
-                a_transpose(i + 1, 0, 1)
-            if c0:
-                relu0(i, 0)
-                g_matmul(i, 1, 0)
-            if c1:
-                h_exit(i + 1, 0, 2)
-                h_exit(i + 1, 0, 3)
-            if c2:
-                exp1(i + 2, 0, 0)
-            if c1:
-                h_matmul(i + 1, 1, 0)
-                h_matmul(i + 1, 1, 1)
-                a_exit(i + 1, 0, 0, True)
-            if c3:
+            if n1:
+                for k in range(8):
+                    h_matmul(i + 1, k // 4, k % 4)
+            if pre:
+                for k in range(4):
+                    a_transpose(LAST, k // 2, k % 2)
+            if n3:
+                mask(i + 3, 0, NT)
+            if not fin:
+                a_quant(i, 1)
+            for t in range(NT):
+                g_matmul(i, t, 0)
+                g_matmul(i, t, 1)
+            if n1:
+                for k in range(8):
+                    h_exit(i + 1, k // 4, k % 4)
+            if pre:
+                a_exit(LAST, 0, 0, True)
+                a_exit(LAST, 0, 1, True)
+                a_exit(LAST, 1, 0, True)
+                a_quant(LAST, 0)
+                a_exit(LAST, 1, 1, True)
+            if n3:
                 level(i + 3, 0, 0, NT)
-            if c1:
-                a_exit(i + 1, 0, 1, True)
-            if c0:
-                finish(i, 0)
-            if c1:
+            if n1:
                 h_quant(i + 1, 0)
-            if c0:
-                relu0(i, 1)
-            if c1:
-                h_exit(i + 1, 1, 0)
-                h_exit(i + 1, 1, 1)
-            if c0:
-                g_matmul(i, 2, 0)
-            if c1:
-                h_matmul(i + 1, 1, 2)
-                a_transpose(i + 1, 0, 2)
-                h_matmul(i + 1, 1, 3)
-            if c0:
-                relu0(i, 2)
-            if c2:
-                exp1(i + 2, 0, 1)
-            if c1:
-                h_exit(i + 1, 1, 2)
-                h_exit(i + 1, 1, 3)
-            if c0:
-                g_matmul(i, 3, 0)
-            if c1:
-                a_transpose(i + 1, 0, 3)
-            if c0:
-                g_matmul(i, 1, 1)
-            if c2:
-                h_matmul(i + 2, 0, 0)
-                h_matmul(i + 2, 0, 1)
-            if c1:
-                a_exit(i + 1, 0, 2, True)
-            if c0:
-                finish(i, 1)
-            if c1:
-                a_exit(i + 1, 0, 3, True)
-                a_transpose(i + 1, 1, 0)
-            if c0:
-                g_matmul(i, 2, 1)
-            if c1:
-                a_transpose(i + 1, 1, 1)
-                a_exit(i + 1, 1, 0, True)
-                a_quant(i + 1, 0)
-            if c0:
-                finish(i, 2)
-            if c3:
-                level(i + 3, 1, 0, NT)
-            if c1:
-                a_exit(i + 1, 1, 1, True)
-                h_quant(i + 1, 1)
-            if c0:
-                relu0(i, 3)
-            if c2:
-                for t in (1, 2, 3):
-                    exp1(i + 2, t, 0)
-                    exp1(i + 2, t, 1)
-            if c1:
-                a_transpose(i + 1, 1, 2)
-                g_matmul(i + 1, 0, 0)
-            if c0:
-                g_matmul(i, 3, 1)
-                finish(i, 3)
-            if c3:
-                level(i + 3, 2, 0, NT)
-            if c1:
-                a_exit(i + 1, 1, 2, True)
-            if c3:
-                level(i + 3, 3, 0, NT)
+            for t in range(NT):
+                relu0(i, t)
+                finish(i, t)
+                if fin:
+                    store(i, t, t + 1)
+                if t == 1 and n1:
+                    h_quant(i + 1, 1)
+                if t == 2 and pre:
+                    a_quant(LAST, 1)
+            if not fin:
+                store(i, 0, NT)

@@ -194,19 +194,18 @@ def tile_rgat_pa_t_kernel(tc, adj, x, dmask, W, out):
                         op1=ALU.add,
                     )
 
-        def a_transpose(b, r, tp):
-            pt = banks.tile([P, 2, 4, P], BF16, tag="bank", name="pt")
-            for tt in range(2):
-                for j in range(4):
-                    nc.tensor.transpose(pt[:, tt, j, :], st[b]["att"][:, r, 2 * tp + tt, P * j : P * j + P], ident_b[:])
-            st[b]["pt%d%d" % (r, tp)] = pt
+        def a_transpose(b, r, t):
+            pt = banks.tile([P, 4, P], BF16, tag="bank", name="pt")
+            for j in range(4):
+                nc.tensor.transpose(pt[:, j, :], st[b]["att"][:, r, t, P * j : P * j + P], ident_b[:])
+            st[b]["pt%d%d" % (r, t)] = pt
 
-        def a_exit(b, r, tp, on_vector):
+        def a_exit(b, r, t, on_vector):
             key = "ag%d" % r
             if key not in st[b]:
                 st[b][key] = two.tile([P, N, 4], BF16, align_bytes=64, name=key)
-            dst = st[b][key][:, 256 * tp : 256 * tp + 256, :].rearrange("p (a n) j -> p a n j", a=2)
-            src = st[b]["pt%d%d" % (r, tp)][:].rearrange("p a j n -> p a n j")
+            dst = st[b][key][:, P * t : P * t + P, :]
+            src = st[b]["pt%d%d" % (r, t)][:].rearrange("p j n -> p n j")
             if on_vector:
                 nc.vector.tensor_copy(out=dst, in_=src)
             else:
@@ -357,8 +356,8 @@ def tile_rgat_pa_t_kernel(tc, adj, x, dmask, W, out):
             if n3:
                 load_x(i + 3)
             if not fin:
-                for k in range(4):
-                    a_transpose(i, k // 2, k % 2)
+                for k in range(8):
+                    a_transpose(i, k // 4, k % 4)
             if n2:
                 x_transpose(i + 2)
             if n1:
@@ -366,9 +365,11 @@ def tile_rgat_pa_t_kernel(tc, adj, x, dmask, W, out):
                     exps(i + 1, t)
             if not fin:
                 a_exit(i, 0, 0, True)
+                a_exit(i, 0, 1, True)
                 if n2:
                     level(i + 2, 1, 0, NT)
-                a_exit(i, 0, 1, True)
+                a_exit(i, 0, 2, True)
+                a_exit(i, 0, 3, True)
                 if n2:
                     level(i + 2, 2, 0, NT)
                 a_quant(i, 0)
@@ -383,16 +384,16 @@ def tile_rgat_pa_t_kernel(tc, adj, x, dmask, W, out):
                 norm(i + 1, 0, i + 1 == LAST)
                 norm(i + 1, 1, i + 1 == LAST)
             if not fin:
-                a_exit(i, 1, 0, False)
-                a_exit(i, 1, 1, False)
+                for t in range(NT):
+                    a_exit(i, 1, t, False)
             if n2:
                 x_quant(i + 2)
             if n1:
                 for k in range(8):
                     h_matmul(i + 1, k // 4, k % 4)
             if pre:
-                for k in range(4):
-                    a_transpose(LAST, k // 2, k % 2)
+                for k in range(8):
+                    a_transpose(LAST, k // 4, k % 4)
             if n3:
                 mask(i + 3, 0, NT)
             if not fin:
@@ -404,11 +405,13 @@ def tile_rgat_pa_t_kernel(tc, adj, x, dmask, W, out):
                 for k in range(8):
                     h_exit(i + 1, k // 4, k % 4)
             if pre:
-                a_exit(LAST, 0, 0, True)
-                a_exit(LAST, 0, 1, True)
+                for t in range(NT):
+                    a_exit(LAST, 0, t, True)
                 a_exit(LAST, 1, 0, True)
-                a_quant(LAST, 0)
                 a_exit(LAST, 1, 1, True)
+                a_quant(LAST, 0)
+                a_exit(LAST, 1, 2, True)
+                a_exit(LAST, 1, 3, True)
             if n3:
                 level(i + 3, 0, 0, NT)
             if n1:

@@ -15,6 +15,7 @@ AX = mybir.AxisListType
 B, N, H, R = 8, 512, 512, 2
 P = 128
 NT = N // P
+LAST = B - 1
 FLOPS = 2 * 2 * B * R * N * N * H
 
 BIG = 3.3895313892515355e38
@@ -34,8 +35,7 @@ def tile_rgat_pa_t_kernel(tc, adj, x, dmask, W, out):
 
         st = [dict() for b in range(B)]
 
-        ident_f = const.tile([P, P], F32)
-        ident_b = const.tile([P, P], BF16)
+        ident = const.tile([P, P], F32)
         dm = const.tile([P, B * N], BF16)
         w_codes = const.tile([P, R, H], U32, align_bytes=64)
         w_scales = const.tile([P, R, H], U8, align_bytes=64)
@@ -55,65 +55,63 @@ def tile_rgat_pa_t_kernel(tc, adj, x, dmask, W, out):
                 )
 
         def load_x(b):
-            xs = three.tile([P, NT * H], BF16, name="xs")
-            nc.sync.dma_start(out=xs[:].rearrange("p (c f) -> p c f", c=NT), in_=x[b].rearrange("(c p) f -> p c f", p=P))
+            xs = three.tile([P, 2, 2 * H], BF16, name="xs")
+            nc.sync.dma_start(out=xs[:], in_=x[b].rearrange("(u p e) f -> p u (e f)", u=2, e=2))
             st[b]["xs"] = xs
 
         def load_a(b, pieces):
-            a = three.tile([P, NT, N * R], BF16, name="a")
+            a = four.tile([P, NT, N * R], BF16, name="a")
             src = adj[b].rearrange("(p t) m r -> p t (m r)", t=NT)
             step = NT // pieces
             for k in range(pieces):
                 nc.sync.dma_start(out=a[:, step * k : step * k + step, :], in_=src[:, step * k : step * k + step, :])
             st[b]["a"] = a
 
-        def make_cap(b, eng):
+        def make_cap(b):
             cap = three.tile([P, N, R], BF16, name="cap")
-            eng.tensor_scalar(
+            nc.vector.tensor_scalar(
                 out=cap[:],
                 in0=dm[:, N * b : N * b + N].unsqueeze(2).to_broadcast([P, N, R]),
-                scalar1=BIG + 1e30,
+                scalar1=BIG,
                 scalar2=NEG,
                 op0=ALU.mult,
                 op1=ALU.add,
             )
             st[b]["cap"] = cap
 
-        def w_group(r):
-            nc.gpsimd.tensor_scalar(
-                out=w_grp[:, r].rearrange("p (c i t) -> p c t i", i=4, t=4),
-                in0=w_raw[:, r].rearrange("p (t c i) -> p c t i", t=4, i=4),
-                scalar1=1.0,
-                scalar2=0.0,
-                op0=ALU.mult,
-                op1=ALU.add,
-            )
+        def w_group(r, eng):
+            src = w_raw[:, r].rearrange("p (t c i) -> p c t i", t=4, i=4)
+            dst = w_grp[:, r].rearrange("p (c i t) -> p c t i", i=4, t=4)
+            if eng == "v":
+                nc.vector.tensor_copy(out=dst, in_=src)
+            else:
+                nc.scalar.copy(out=dst, in_=src)
 
         def w_quant(r):
             nc.vector.quantize_mx(out=w_codes[:, r, :].bitcast(FP8X4), scales=w_scales[:, r, :], in_=w_grp[:, r])
 
-        def x_transpose(b):
-            xw = st[b]["xs"][:].bitcast(F32)
-            st[b]["xt"] = []
-            for cp in range(2):
-                xt = banks.tile([P, 2, 256], F32, tag="bank", name="xt")
-                for cc in range(2):
-                    c = 2 * cp + cc
-                    for u in range(2):
-                        nc.tensor.transpose(
-                            xt[:, u, P * cc : P * cc + P], xw[:, 256 * c + P * u : 256 * c + P * u + P], ident_f[:]
-                        )
-                st[b]["xt"].append(xt)
-
-        def x_exit(b, cp, on_vector):
-            if cp == 0:
-                st[b]["xg"] = two.tile([P, N * 4], BF16, align_bytes=64, name="xg")
-            dst = st[b]["xg"][:].bitcast(F32).rearrange("p (n u) -> p n u", u=2)[:, 256 * cp : 256 * cp + 256, :]
-            src = st[b]["xt"][cp][:].rearrange("p u n -> p n u")
-            if on_vector:
+        def words_exit(dst, bank, eng):
+            src = bank[:].rearrange("p u n -> p n u")
+            if eng == "v":
                 nc.vector.tensor_copy(out=dst, in_=src)
             else:
                 nc.scalar.copy(out=dst, in_=src)
+
+        def x_transpose(b):
+            st[b]["xt"] = []
+            for uu in range(2):
+                xt = banks.tile([P, 2, 256], F32, tag="bank", name="xt")
+                for e in range(2):
+                    xw = st[b]["xs"][:, uu, H * e : H * e + H].bitcast(F32)
+                    for u in range(2):
+                        nc.tensor.transpose(xt[:, u, P * e : P * e + P], xw[:, P * u : P * u + P], ident[:])
+                st[b]["xt"].append(xt)
+
+        def x_exit(b, k, eng):
+            if k == 0:
+                st[b]["xg"] = two.tile([P, N * 4], BF16, align_bytes=64, name="xg")
+            dst = st[b]["xg"][:].bitcast(F32).rearrange("p (n u) -> p n u", u=2)[:, 256 * k : 256 * k + 256, :]
+            words_exit(dst, st[b]["xt"][k], eng)
 
         def x_quant(b):
             x_codes = two.tile([P, N], U32, align_bytes=64, name="x_codes")
@@ -122,11 +120,8 @@ def tile_rgat_pa_t_kernel(tc, adj, x, dmask, W, out):
             st[b]["xc"] = (x_codes, x_scales)
 
         def mask(b, t0, t1):
-            if t0 == 0:
-                st[b]["lg"] = two.tile([P, NT, N * R], BF16, name="lg")
-                st[b]["nmx"] = three.tile([P, NT, R], F32, name="nmx")
             nc.vector.tensor_tensor(
-                out=st[b]["lg"][:, t0:t1, :],
+                out=st[b]["a"][:, t0:t1, :],
                 in0=st[b]["a"][:, t0:t1, :],
                 in1=st[b]["cap"][:].rearrange("p m r -> p (m r)").unsqueeze(1).to_broadcast([P, t1 - t0, N * R]),
                 op=ALU.min,
@@ -134,14 +129,12 @@ def tile_rgat_pa_t_kernel(tc, adj, x, dmask, W, out):
 
         def level(b, j, t0, t1):
             key = "lv%d" % t0
-            if j == 0:
-                cur = st[b]["lg"][:, t0:t1, :]
-            else:
-                cur = st[b][key]
+            if "nmx" not in st[b]:
+                st[b]["nmx"] = three.tile([P, NT, R], F32, name="nmx")
+            cur = st[b]["a"][:, t0:t1, :] if j == 0 else st[b][key]
             if j < 4:
                 width = 512 // (2 ** j)
-                slot = 2 if t1 - t0 == NT else t0 % 2
-                nxt = one.tile([P, t1 - t0, width], BF16, name="tree%d_%d" % (width, slot))
+                nxt = one.tile([P, t1 - t0, width], BF16, name="tree%d_%d" % (width, 2 if t1 - t0 == NT else t0 // 2))
                 nc.vector.tensor_tensor(out=nxt[:], in0=cur[:, :, 0:width], in1=cur[:, :, width : 2 * width], op=ALU.max)
                 st[b][key] = nxt[:]
             else:
@@ -157,11 +150,11 @@ def tile_rgat_pa_t_kernel(tc, adj, x, dmask, W, out):
             if t == 0:
                 st[b]["e"] = two.tile([P, NT, R, N], F32, tag="e", name="e", align_bytes=64)
                 st[b]["ssum"] = three.tile([P, NT, R], F32, name="ssum")
-            lg_t = st[b]["lg"][:, t, :].rearrange("p (m r) -> p m r", r=R)
+            row = st[b]["a"][:, t, :].rearrange("p (m r) -> p m r", r=R)
             for r in range(R):
                 nc.scalar.activation(
                     out=st[b]["e"][:, t, r, :],
-                    in_=lg_t[:, :, r],
+                    in_=row[:, :, r],
                     func=ACT.Exp,
                     bias=st[b]["nmx"][:, t, r : r + 1],
                     scale=1.0,
@@ -174,49 +167,34 @@ def tile_rgat_pa_t_kernel(tc, adj, x, dmask, W, out):
             st[b]["rs"] = rs
             st[b]["att"] = two.tile([P, R, NT, N], BF16, name="att")
 
-        def norm(b, r, on_vector):
-            for t in range(NT):
-                if on_vector:
-                    nc.vector.tensor_scalar(
-                        out=st[b]["att"][:, r, t, :],
-                        in0=st[b]["e"][:, t, r, :],
-                        scalar1=st[b]["rs"][:, t, r : r + 1],
-                        scalar2=None,
-                        op0=ALU.mult,
-                    )
-                else:
-                    nc.gpsimd.tensor_scalar(
-                        out=st[b]["att"][:, r, t, :],
-                        in0=st[b]["e"][:, t, r, :],
-                        scalar1=st[b]["rs"][:, t, r : r + 1],
-                        scalar2=0.0,
-                        op0=ALU.mult,
-                        op1=ALU.add,
-                    )
+        def norm(b, r, t):
+            nc.vector.tensor_scalar(
+                out=st[b]["att"][:, r, t, :],
+                in0=st[b]["e"][:, t, r, :],
+                scalar1=st[b]["rs"][:, t, r : r + 1],
+                scalar2=None,
+                op0=ALU.mult,
+            )
 
-        def a_transpose(b, r, t):
-            pt = banks.tile([P, 4, P], BF16, tag="bank", name="pt")
-            for j in range(4):
-                nc.tensor.transpose(pt[:, j, :], st[b]["att"][:, r, t, P * j : P * j + P], ident_b[:])
-            st[b]["pt%d%d" % (r, t)] = pt
+        def a_transpose(b, r, k):
+            pt = banks.tile([P, 2, 256], F32, tag="bank", name="pt")
+            for tt in range(2):
+                aw = st[b]["att"][:, r, 2 * k + tt, :].bitcast(F32)
+                for u in range(2):
+                    nc.tensor.transpose(pt[:, u, P * tt : P * tt + P], aw[:, P * u : P * u + P], ident[:])
+            st[b]["pt%d%d" % (r, k)] = pt
 
-        def a_exit(b, r, t, on_vector):
+        def a_exit(b, r, k, eng):
             key = "ag%d" % r
             if key not in st[b]:
-                st[b][key] = two.tile([P, N, 4], BF16, align_bytes=64, name=key)
-            dst = st[b][key][:, P * t : P * t + P, :]
-            src = st[b]["pt%d%d" % (r, t)][:].rearrange("p j n -> p n j")
-            if on_vector:
-                nc.vector.tensor_copy(out=dst, in_=src)
-            else:
-                nc.scalar.copy(out=dst, in_=src)
+                st[b][key] = two.tile([P, N * 4], BF16, align_bytes=64, name=key)
+            dst = st[b][key][:].bitcast(F32).rearrange("p (n u) -> p n u", u=2)[:, 256 * k : 256 * k + 256, :]
+            words_exit(dst, st[b]["pt%d%d" % (r, k)], eng)
 
         def a_quant(b, r):
             codes = two.tile([P, N], U32, align_bytes=64, name="a_codes%d" % r)
             scales = two.tile([P, N], U8, align_bytes=64, name="a_scales%d" % r)
-            nc.vector.quantize_mx(
-                out=codes[:].bitcast(FP8X4), scales=scales[:], in_=st[b]["ag%d" % r][:].rearrange("p n j -> p (n j)")
-            )
+            nc.vector.quantize_mx(out=codes[:].bitcast(FP8X4), scales=scales[:], in_=st[b]["ag%d" % r][:])
             st[b]["ac%d" % r] = (codes, scales)
 
         def h_matmul(b, r, og):
@@ -234,13 +212,16 @@ def tile_rgat_pa_t_kernel(tc, adj, x, dmask, W, out):
                 )
             st[b]["ph%d%d" % (r, og)] = ph
 
-        def h_exit(b, r, og):
+        def h_exit(b, r, og, eng):
             key = "hg%d" % r
             if key not in st[b]:
                 st[b][key] = two.tile([P, H, 4], BF16, align_bytes=64, name=key)
-            nc.scalar.copy(
-                out=st[b][key][:, P * og : P * og + P, :], in_=st[b]["ph%d%d" % (r, og)][:].rearrange("p c o -> p o c")
-            )
+            dst = st[b][key][:, P * og : P * og + P, :]
+            src = st[b]["ph%d%d" % (r, og)][:].rearrange("p c o -> p o c")
+            if eng == "v":
+                nc.vector.tensor_copy(out=dst, in_=src)
+            else:
+                nc.scalar.copy(out=dst, in_=src)
 
         def h_quant(b, r):
             codes = two.tile([P, H], U32, align_bytes=64, name="h_codes%d" % r)
@@ -284,146 +265,128 @@ def tile_rgat_pa_t_kernel(tc, adj, x, dmask, W, out):
 
         out_v = [out[b].rearrange("(p t) o -> p t o", t=NT) for b in range(B)]
 
-        LAST = B - 1
-
         def store(b, t0, t1):
             nc.sync.dma_start(out=out_v[b][:, t0:t1, :], in_=st[b]["ot"][:, t0:t1, :])
 
-        make_identity(nc, ident_f[:])
+        make_identity(nc, ident[:])
         load_mask(0, N)
         load_a(0, NT)
         load_w(0)
-        load_w(1)
         load_x(0)
+        load_w(1)
         load_mask(N, B * N)
-        for b in (1, 2):
-            load_a(b, 1)
-            load_x(b)
-        make_cap(0, nc.vector)
-        make_cap(1, nc.gpsimd)
-        w_group(0)
-        w_group(1)
-        make_identity(nc, ident_b[:])
-        make_cap(2, nc.gpsimd)
-        for t in (0, 2):
-            mask(0, t, t + 1)
-            mask(0, t + 1, t + 2)
+        load_a(1, 1)
+        load_x(1)
+        load_a(2, 1)
+        make_cap(0)
+        for t0 in (0, 2):
+            mask(0, t0, t0 + 1)
+            mask(0, t0 + 1, t0 + 2)
             for j in range(5):
-                level(0, j, t, t + 1)
-                level(0, j, t + 1, t + 2)
-            exps(0, t)
-            exps(0, t + 1)
-            if t == 0:
+                level(0, j, t0, t0 + 2)
+            exps(0, t0)
+            exps(0, t0 + 1)
+            if t0 == 0:
+                w_group(0, "v")
+                w_group(1, "s")
                 x_transpose(0)
-                x_exit(0, 0, False)
-                x_exit(0, 1, False)
-        load_a(3, 1)
-        make_cap(3, nc.gpsimd)
-        w_quant(0)
+                x_exit(0, 0, "s")
+                x_exit(0, 1, "s")
+                w_quant(0)
+        make_cap(1)
         x_quant(0)
-        recip(0)
-        mask(1, 0, NT)
         w_quant(1)
-        norm(0, 0, False)
-        norm(0, 1, False)
-        x_transpose(1)
-        for k in range(8):
-            h_matmul(0, k // 4, k % 4)
-        level(1, 0, 0, NT)
-        x_exit(1, 0, True)
-        level(1, 1, 0, NT)
-        x_exit(1, 1, True)
-        level(1, 2, 0, NT)
-        x_quant(1)
-        level(1, 3, 0, NT)
-        level(1, 4, 0, NT)
-        for k in range(8):
-            h_exit(0, k // 4, k % 4)
-        mask(2, 0, NT)
-        h_quant(0, 0)
-        level(2, 0, 0, NT)
-        h_quant(0, 1)
+        for k in range(4):
+            h_matmul(0, 0, k)
+        make_cap(2)
+        mask(1, 0, 2)
+        mask(1, 2, 4)
+        for j in range(5):
+            level(1, j, 0, NT)
 
-        for i in range(B):
-            pre = i == LAST - 1
-            fin = i == LAST
-            n1 = i + 1 < B
-            n2 = i + 2 < B
-            n3 = i + 3 < B
+        for i in range(-1, B):
+            cur, n1, n2, n3 = i >= 0, i + 1 < B, i + 2 < B, i + 3 < B
             if i + 4 < B:
                 load_a(i + 4, 1)
-                make_cap(i + 4, nc.gpsimd)
             if n3:
                 load_x(i + 3)
-            if not fin:
-                for k in range(8):
-                    a_transpose(i, k // 4, k % 4)
-            if n2:
-                x_transpose(i + 2)
-            if n1:
-                for t in range(NT):
-                    exps(i + 1, t)
-            if not fin:
-                a_exit(i, 0, 0, True)
-                a_exit(i, 0, 1, True)
-                if n2:
-                    level(i + 2, 1, 0, NT)
-                a_exit(i, 0, 2, True)
-                a_exit(i, 0, 3, True)
-                if n2:
-                    level(i + 2, 2, 0, NT)
-                a_quant(i, 0)
-                if n2:
-                    level(i + 2, 3, 0, NT)
-            if n2:
-                x_exit(i + 2, 0, True)
-                level(i + 2, 4, 0, NT)
-                x_exit(i + 2, 1, True)
+            if cur:
+                for r in range(R):
+                    for k in range(2):
+                        a_transpose(i, r, k)
+            if n1 and i >= 0:
+                for k in range(4):
+                    h_matmul(i + 1, 0, k)
+            if cur:
+                for r in range(R):
+                    for k in range(2):
+                        a_exit(i, r, k, "s")
             if n1:
                 recip(i + 1)
-                norm(i + 1, 0, i + 1 == LAST)
-                norm(i + 1, 1, i + 1 == LAST)
-            if not fin:
-                for t in range(NT):
-                    a_exit(i, 1, t, False)
-            if n2:
-                x_quant(i + 2)
+                norm(i + 1, 0, 0)
+                norm(i + 1, 0, 1)
+            if cur:
+                a_quant(i, 0)
             if n1:
-                for k in range(8):
-                    h_matmul(i + 1, k // 4, k % 4)
-            if pre:
-                for k in range(8):
-                    a_transpose(LAST, k // 4, k % 4)
-            if n3:
-                mask(i + 3, 0, NT)
-            if not fin:
+                norm(i + 1, 0, 2)
+                norm(i + 1, 0, 3)
+                norm(i + 1, 1, 0)
+            if cur:
                 a_quant(i, 1)
-            for t in range(NT):
-                g_matmul(i, t, 0)
-                g_matmul(i, t, 1)
             if n1:
-                for k in range(8):
-                    h_exit(i + 1, k // 4, k % 4)
-            if pre:
-                for t in range(NT):
-                    a_exit(LAST, 0, t, True)
-                a_exit(LAST, 1, 0, True)
-                a_exit(LAST, 1, 1, True)
-                a_quant(LAST, 0)
-                a_exit(LAST, 1, 2, True)
-                a_exit(LAST, 1, 3, True)
+                norm(i + 1, 1, 1)
+                norm(i + 1, 1, 2)
+                norm(i + 1, 1, 3)
+                for k in range(4):
+                    h_exit(i + 1, 0, k, "s")
             if n3:
-                level(i + 3, 0, 0, NT)
+                mask(i + 3, 0, 2)
             if n1:
                 h_quant(i + 1, 0)
-            for t in range(NT):
-                relu0(i, t)
-                finish(i, t)
-                if fin:
-                    store(i, t, t + 1)
-                if t == 1 and n1:
-                    h_quant(i + 1, 1)
-                if t == 2 and pre:
-                    a_quant(LAST, 1)
-            if not fin:
+            if cur:
+                for t in range(NT):
+                    g_matmul(i, t, 0)
+                    g_matmul(i, t, 1)
+                for t in range(NT):
+                    relu0(i, t)
+            if n1:
+                for k in range(4):
+                    h_matmul(i + 1, 1, k)
+            if n2:
+                x_transpose(i + 2)
+            if cur:
+                finish(i, 0)
+            if n3:
+                mask(i + 3, 2, 4)
+            if cur:
+                finish(i, 1)
+            if n3:
+                level(i + 3, 0, 0, NT)
+            if cur:
+                finish(i, 2)
+            if n3:
+                level(i + 3, 1, 0, NT)
+            if cur:
+                finish(i, 3)
                 store(i, 0, NT)
+            if n3:
+                level(i + 3, 2, 0, NT)
+            if n1:
+                for k in range(4):
+                    h_exit(i + 1, 1, k, "s")
+            if n2:
+                x_exit(i + 2, 0, "v")
+            if n3:
+                level(i + 3, 3, 0, NT)
+            if n2:
+                x_exit(i + 2, 1, "v")
+            if n3:
+                level(i + 3, 4, 0, NT)
+            if n1:
+                h_quant(i + 1, 1)
+            if n2:
+                x_quant(i + 2)
+                for t in range(NT):
+                    exps(i + 2, t)
+            if i + 4 < B:
+                make_cap(i + 4)

@@ -15,6 +15,8 @@ AX = mybir.AxisListType
 B, N, H, R = 8, 512, 512, 2
 P = 128
 NT = N // P
+NQ = R * NT
+NV = 2
 LAST = B - 1
 FLOPS = 2 * 2 * B * R * N * N * H
 
@@ -44,8 +46,8 @@ def tile_rgat_pa_t_kernel(tc, adj, x, dmask, W, out):
         w_grp = w_stage[:, 1]
         dm_row = dmask.rearrange("b o m -> (b o m)")
 
-        def load_mask(lo, hi):
-            nc.scalar.dma_start(out=dm[:, lo:hi], in_=dm_row[lo:hi].partition_broadcast(P))
+        def load_mask(b, queue):
+            queue.dma_start(out=dm[:, N * b : N * b + N], in_=dm_row[N * b : N * b + N].partition_broadcast(P))
 
         def load_w(r):
             for u in range(2):
@@ -59,13 +61,11 @@ def tile_rgat_pa_t_kernel(tc, adj, x, dmask, W, out):
             nc.sync.dma_start(out=xs[:], in_=x[b].rearrange("(u p e) f -> p u (e f)", u=2, e=2))
             st[b]["xs"] = xs
 
-        def load_a(b, pieces):
-            a = four.tile([P, NT, N * R], BF16, name="a")
+        def load_a(b, t0, t1):
+            if t0 == 0:
+                st[b]["a"] = four.tile([P, NT, N * R], BF16, name="a")
             src = adj[b].rearrange("(p t) m r -> p t (m r)", t=NT)
-            step = NT // pieces
-            for k in range(pieces):
-                nc.sync.dma_start(out=a[:, step * k : step * k + step, :], in_=src[:, step * k : step * k + step, :])
-            st[b]["a"] = a
+            nc.sync.dma_start(out=st[b]["a"][:, t0:t1, :], in_=src[:, t0:t1, :])
 
         def make_cap(b):
             cap = three.tile([P, N, R], BF16, name="cap")
@@ -134,7 +134,7 @@ def tile_rgat_pa_t_kernel(tc, adj, x, dmask, W, out):
             cur = st[b]["a"][:, t0:t1, :] if j == 0 else st[b][key]
             if j < 4:
                 width = 512 // (2 ** j)
-                nxt = one.tile([P, t1 - t0, width], BF16, name="tree%d_%d" % (width, 2 if t1 - t0 == NT else t0 // 2))
+                nxt = one.tile([P, t1 - t0, width], BF16, name="tree%d_%d" % (width, NT if t1 - t0 == NT else t0 % 2))
                 nc.vector.tensor_tensor(out=nxt[:], in0=cur[:, :, 0:width], in1=cur[:, :, width : 2 * width], op=ALU.max)
                 st[b][key] = nxt[:]
             else:
@@ -149,7 +149,8 @@ def tile_rgat_pa_t_kernel(tc, adj, x, dmask, W, out):
         def exps(b, t):
             if t == 0:
                 st[b]["e"] = two.tile([P, NT, R, N], F32, tag="e", name="e", align_bytes=64)
-                st[b]["ssum"] = three.tile([P, NT, R], F32, name="ssum")
+                st[b]["ssum"] = three.tile([P, R * NT], F32, name="ssum")
+                st[b]["att"] = two.tile([P, R, NT, N], BF16, name="att")
             row = st[b]["a"][:, t, :].rearrange("p (m r) -> p m r", r=R)
             for r in range(R):
                 nc.scalar.activation(
@@ -158,23 +159,24 @@ def tile_rgat_pa_t_kernel(tc, adj, x, dmask, W, out):
                     func=ACT.Exp,
                     bias=st[b]["nmx"][:, t, r : r + 1],
                     scale=1.0,
-                    accum_out=st[b]["ssum"][:, t, r : r + 1],
+                    accum_out=st[b]["ssum"][:, NT * r + t : NT * r + t + 1],
                 )
 
-        def recip(b):
-            rs = three.tile([P, NT, R], F32, name="rs")
-            nc.vector.reciprocal(out=rs[:], in_=st[b]["ssum"][:])
-            st[b]["rs"] = rs
-            st[b]["att"] = two.tile([P, R, NT, N], BF16, name="att")
+        def recip(b, lo, hi):
+            rs = three.tile([P, R * NT], F32, name="rs%d" % lo)
+            nc.vector.reciprocal(out=rs[:, lo:hi], in_=st[b]["ssum"][:, lo:hi])
+            for q in range(lo, hi):
+                st[b]["rs%d" % q] = rs
 
-        def norm(b, r, t):
-            nc.vector.tensor_scalar(
-                out=st[b]["att"][:, r, t, :],
-                in0=st[b]["e"][:, t, r, :],
-                scalar1=st[b]["rs"][:, t, r : r + 1],
-                scalar2=None,
-                op0=ALU.mult,
-            )
+        def norm(b, q, eng):
+            r, t = q // NT, q % NT
+            dst = st[b]["att"][:, r, t, :]
+            src = st[b]["e"][:, t, r, :]
+            scale = st[b]["rs%d" % q][:, q : q + 1]
+            if eng == "v":
+                nc.vector.tensor_scalar(out=dst, in0=src, scalar1=scale, scalar2=None, op0=ALU.mult)
+            else:
+                nc.gpsimd.tensor_scalar(out=dst, in0=src, scalar1=scale, scalar2=0.0, op0=ALU.mult, op1=ALU.add)
 
         def a_transpose(b, r, k):
             pt = banks.tile([P, 2, 256], F32, tag="bank", name="pt")
@@ -191,11 +193,15 @@ def tile_rgat_pa_t_kernel(tc, adj, x, dmask, W, out):
             dst = st[b][key][:].bitcast(F32).rearrange("p (n u) -> p n u", u=2)[:, 256 * k : 256 * k + 256, :]
             words_exit(dst, st[b]["pt%d%d" % (r, k)], eng)
 
-        def a_quant(b, r):
-            codes = two.tile([P, N], U32, align_bytes=64, name="a_codes%d" % r)
-            scales = two.tile([P, N], U8, align_bytes=64, name="a_scales%d" % r)
-            nc.vector.quantize_mx(out=codes[:].bitcast(FP8X4), scales=scales[:], in_=st[b]["ag%d" % r][:])
-            st[b]["ac%d" % r] = (codes, scales)
+        def a_quant(b, r, lo, hi):
+            if lo == 0:
+                codes = two.tile([P, N], U32, align_bytes=64, name="a_codes%d" % r)
+                scales = two.tile([P, N], U8, align_bytes=64, name="a_scales%d" % r)
+                st[b]["ac%d" % r] = (codes, scales)
+            codes, scales = st[b]["ac%d" % r]
+            nc.vector.quantize_mx(
+                out=codes[:, lo:hi].bitcast(FP8X4), scales=scales[:, lo:hi], in_=st[b]["ag%d" % r][:, 4 * lo : 4 * hi]
+            )
 
         def h_matmul(b, r, og):
             ph = banks.tile([P, NT, P], F32, tag="bank", name="ph")
@@ -269,124 +275,151 @@ def tile_rgat_pa_t_kernel(tc, adj, x, dmask, W, out):
             nc.sync.dma_start(out=out_v[b][:, t0:t1, :], in_=st[b]["ot"][:, t0:t1, :])
 
         make_identity(nc, ident[:])
-        load_mask(0, N)
-        load_a(0, NT)
-        load_w(0)
+        load_mask(0, nc.scalar)
+        load_a(0, 0, 1)
+        load_a(0, 1, 2)
         load_x(0)
+        load_w(0)
+        load_a(0, 2, 4)
         load_w(1)
-        load_mask(N, B * N)
-        load_a(1, 1)
-        load_x(1)
-        load_a(2, 1)
-        make_cap(0)
-        for t0 in (0, 2):
-            mask(0, t0, t0 + 1)
-            mask(0, t0 + 1, t0 + 2)
+        for b in (1, 2, 3):
+            load_mask(b, nc.sync)
+            load_a(b, 0, NT)
+            if b < 3:
+                load_x(b)
+
+        def woven_tree(b, t):
+            mask(b, t, t + 1)
+            mask(b, t + 1, t + 2)
             for j in range(5):
-                level(0, j, t0, t0 + 2)
-            exps(0, t0)
-            exps(0, t0 + 1)
-            if t0 == 0:
-                w_group(0, "v")
-                w_group(1, "s")
-                x_transpose(0)
-                x_exit(0, 0, "s")
-                x_exit(0, 1, "s")
-                w_quant(0)
-        make_cap(1)
+                level(b, j, t, t + 1)
+                level(b, j, t + 1, t + 2)
+
+        make_cap(0)
+        woven_tree(0, 0)
+        x_transpose(0)
+        x_exit(0, 0, "s")
+        x_exit(0, 1, "s")
+        exps(0, 0)
+        exps(0, 1)
+        w_group(0, "v")
+        w_group(1, "s")
         x_quant(0)
-        w_quant(1)
+        w_quant(0)
         for k in range(4):
             h_matmul(0, 0, k)
-        make_cap(2)
+        woven_tree(0, 2)
+        exps(0, 2)
+        exps(0, 3)
+        make_cap(1)
         mask(1, 0, 2)
+        w_quant(1)
+        for k in range(4):
+            h_exit(0, 0, k, "s")
+        for k in range(4):
+            h_matmul(0, 1, k)
+        x_transpose(1)
+        for k in range(4):
+            h_exit(0, 1, k, "s")
         mask(1, 2, 4)
+        recip(0, 0, NQ)
         for j in range(5):
             level(1, j, 0, NT)
+            if j < 4:
+                norm(0, j, "v")
+        for t in range(NT):
+            exps(1, t)
+        for q in range(4, NQ):
+            norm(0, q, "v")
+        x_exit(1, 0, "v")
+        x_exit(1, 1, "v")
+        h_quant(0, 0)
+        x_quant(1)
+        h_quant(0, 1)
+        make_cap(2)
 
-        for i in range(-1, B):
-            cur, n1, n2, n3 = i >= 0, i + 1 < B, i + 2 < B, i + 3 < B
+        for i in range(B):
+            n1, n2, fin = i + 1 < B, i + 2 < B, i == LAST
             if i + 4 < B:
-                load_a(i + 4, 1)
-            if n3:
+                load_mask(i + 4, nc.sync)
+                load_a(i + 4, 0, NT)
+            if i + 3 < B:
                 load_x(i + 3)
-            if cur:
-                for r in range(R):
-                    for k in range(2):
-                        a_transpose(i, r, k)
-            if n1 and i >= 0:
+            for r in range(R):
+                for k in range(2):
+                    a_transpose(i, r, k)
+            if n1:
                 for k in range(4):
                     h_matmul(i + 1, 0, k)
-            if cur:
+            if n2:
+                mask(i + 2, 0, 2)
+            elif n1:
+                h_exit(i + 1, 0, 0, "v")
+                h_exit(i + 1, 0, 1, "v")
+            if n1:
+                recip(i + 1, 0, NV)
+            if n2:
+                mask(i + 2, 2, 4)
+            if fin:
+                a_exit(i, 0, 0, "s")
+                a_exit(i, 1, 0, "v")
+                a_exit(i, 0, 1, "s")
+                a_exit(i, 1, 1, "s")
+                for k in range(2):
+                    for r in range(R):
+                        a_quant(i, r, 256 * k, 256 * k + 256)
+            else:
                 for r in range(R):
                     for k in range(2):
                         a_exit(i, r, k, "s")
+                a_quant(i, 0, 0, N)
+            if n2:
+                level(i + 2, 0, 0, NT)
+            elif n1:
+                norm(i + 1, 0, "v")
+            if not fin:
+                a_quant(i, 1, 0, N)
             if n1:
-                recip(i + 1)
-                norm(i + 1, 0, 0)
-                norm(i + 1, 0, 1)
-            if cur:
-                a_quant(i, 0)
-            if n1:
-                norm(i + 1, 0, 2)
-                norm(i + 1, 0, 3)
-                norm(i + 1, 1, 0)
-            if cur:
-                a_quant(i, 1)
-            if n1:
-                norm(i + 1, 1, 1)
-                norm(i + 1, 1, 2)
-                norm(i + 1, 1, 3)
-                for k in range(4):
+                for k in range(0 if n2 else 2, 4):
                     h_exit(i + 1, 0, k, "s")
-            if n3:
-                mask(i + 3, 0, 2)
+            if n2:
+                level(i + 2, 1, 0, NT)
+                norm(i + 1, 0, "v")
+                level(i + 2, 2, 0, NT)
             if n1:
-                h_quant(i + 1, 0)
-            if cur:
-                for t in range(NT):
-                    g_matmul(i, t, 0)
-                    g_matmul(i, t, 1)
-                for t in range(NT):
-                    relu0(i, t)
+                norm(i + 1, 1, "v")
+                recip(i + 1, NV, NQ)
+                for q in range(NV, NQ):
+                    norm(i + 1, q, "g")
+            for t in range(NT):
+                g_matmul(i, t, 0)
+                g_matmul(i, t, 1)
+            for t in range(NT):
+                relu0(i, t)
+                finish(i, t)
+                if n2 and t < 2:
+                    level(i + 2, 3 + t, 0, NT)
+                if fin:
+                    store(i, t, t + 1)
+            if not fin:
+                store(i, 0, NT)
             if n1:
                 for k in range(4):
                     h_matmul(i + 1, 1, k)
+                for k in range(4):
+                    h_exit(i + 1, 1, k, "v" if k == 0 else "s")
             if n2:
                 x_transpose(i + 2)
-            if cur:
-                finish(i, 0)
-            if n3:
-                mask(i + 3, 2, 4)
-            if cur:
-                finish(i, 1)
-            if n3:
-                level(i + 3, 0, 0, NT)
-            if cur:
-                finish(i, 2)
-            if n3:
-                level(i + 3, 1, 0, NT)
-            if cur:
-                finish(i, 3)
-                store(i, 0, NT)
-            if n3:
-                level(i + 3, 2, 0, NT)
-            if n1:
-                for k in range(4):
-                    h_exit(i + 1, 1, k, "s")
-            if n2:
                 x_exit(i + 2, 0, "v")
-            if n3:
-                level(i + 3, 3, 0, NT)
-            if n2:
                 x_exit(i + 2, 1, "v")
-            if n3:
-                level(i + 3, 4, 0, NT)
+            if n1:
+                h_quant(i + 1, 0)
+            if i + 3 < B:
+                make_cap(i + 3)
+            if n2:
+                x_quant(i + 2)
             if n1:
                 h_quant(i + 1, 1)
             if n2:
-                x_quant(i + 2)
                 for t in range(NT):
                     exps(i + 2, t)
-            if i + 4 < B:
-                make_cap(i + 4)

@@ -388,17 +388,20 @@ def tile_rgat_pa_t_kernel(tc, adj, x, dmask, W, out):
                 level(i + 2, 2, 0, NT)
             if n1:
                 norm(i + 1, 1, "v")
+            if n2:
+                level(i + 2, 3, 0, NT)
+            if n1:
                 recip(i + 1, NV, NQ)
                 for q in range(NV, NQ):
                     norm(i + 1, q, "g")
-            for t in range(NT):
-                g_matmul(i, t, 0)
-                g_matmul(i, t, 1)
+            for r in range(R):
+                for t in range(NT):
+                    g_matmul(i, t, r)
             for t in range(NT):
                 relu0(i, t)
                 finish(i, t)
-                if n2 and t < 2:
-                    level(i + 2, 3 + t, 0, NT)
+                if n2 and t == 0:
+                    level(i + 2, 4, 0, NT)
                 if fin:
                     store(i, t, t + 1)
             if not fin:

@@ -16,7 +16,7 @@ B, N, H, R = 8, 512, 512, 2
 P = 128
 NT = N // P
 NQ = R * NT
-NV = 2
+NV = 4
 LAST = B - 1
 FLOPS = 2 * 2 * B * R * N * N * H
 
@@ -417,11 +417,13 @@ def tile_rgat_pa_t_kernel(tc, adj, x, dmask, W, out):
                 x_exit(i + 2, 1, "v")
             if n1:
                 h_quant(i + 1, 0)
+                norm(i + 1, 2, "v")
             if i + 3 < B:
                 make_cap(i + 3)
             if n2:
                 x_quant(i + 2)
             if n1:
+                norm(i + 1, 3, "v")
                 h_quant(i + 1, 1)
             if n2:
                 for t in range(NT):

@@ -20,8 +20,8 @@ NV = 4
 LAST = B - 1
 FLOPS = 2 * 2 * B * R * N * N * H
 
-BIG = 3.3895313892515355e38
-NEG = -1e30
+OPEN = 3.3961513649220713e38
+SHUT = -1.004922760984937e30
 
 
 def tile_rgat_pa_t_kernel(tc, adj, x, dmask, W, out):
@@ -68,14 +68,9 @@ def tile_rgat_pa_t_kernel(tc, adj, x, dmask, W, out):
             nc.sync.dma_start(out=st[b]["a"][:, t0:t1, :], in_=src[:, t0:t1, :])
 
         def make_cap(b):
-            cap = three.tile([P, N, R], BF16, name="cap")
+            cap = three.tile([P, N], F32, name="cap")
             nc.vector.tensor_scalar(
-                out=cap[:],
-                in0=dm[:, N * b : N * b + N].unsqueeze(2).to_broadcast([P, N, R]),
-                scalar1=BIG,
-                scalar2=NEG,
-                op0=ALU.mult,
-                op1=ALU.add,
+                out=cap[:], in0=dm[:, N * b : N * b + N], scalar1=OPEN, scalar2=SHUT, op0=ALU.mult, op1=ALU.add
             )
             st[b]["cap"] = cap
 
@@ -108,7 +103,7 @@ def tile_rgat_pa_t_kernel(tc, adj, x, dmask, W, out):
                 st[b]["xt"].append(xt)
 
         def x_exit(b, k, eng):
-            if k == 0:
+            if "xg" not in st[b]:
                 st[b]["xg"] = two.tile([P, N * 4], BF16, align_bytes=64, name="xg")
             dst = st[b]["xg"][:].bitcast(F32).rearrange("p (n u) -> p n u", u=2)[:, 256 * k : 256 * k + 256, :]
             words_exit(dst, st[b]["xt"][k], eng)
@@ -123,7 +118,7 @@ def tile_rgat_pa_t_kernel(tc, adj, x, dmask, W, out):
             nc.vector.tensor_tensor(
                 out=st[b]["a"][:, t0:t1, :],
                 in0=st[b]["a"][:, t0:t1, :],
-                in1=st[b]["cap"][:].rearrange("p m r -> p (m r)").unsqueeze(1).to_broadcast([P, t1 - t0, N * R]),
+                in1=st[b]["cap"][:].bitcast(BF16).unsqueeze(1).to_broadcast([P, t1 - t0, N * R]),
                 op=ALU.min,
             )
 
@@ -258,7 +253,7 @@ def tile_rgat_pa_t_kernel(tc, adj, x, dmask, W, out):
             st[b]["g0s%d" % t] = g0
 
         def finish(b, t):
-            if t == 0:
+            if "ot" not in st[b]:
                 st[b]["ot"] = two.tile([P, NT, H], F32, name="ot")
             nc.vector.scalar_tensor_tensor(
                 out=st[b]["ot"][:, t, :],
@@ -314,12 +309,12 @@ def tile_rgat_pa_t_kernel(tc, adj, x, dmask, W, out):
         make_cap(1)
         mask(1, 0, 2)
         w_quant(1)
-        for k in range(4):
+        for k in reversed(range(4)):
             h_exit(0, 0, k, "s")
         for k in range(4):
             h_matmul(0, 1, k)
         x_transpose(1)
-        for k in range(4):
+        for k in reversed(range(4)):
             h_exit(0, 1, k, "s")
         mask(1, 2, 4)
         recip(0, 0, NQ)
@@ -370,7 +365,7 @@ def tile_rgat_pa_t_kernel(tc, adj, x, dmask, W, out):
                         a_quant(i, r, 256 * k, 256 * k + 256)
             else:
                 for r in range(R):
-                    for k in range(2):
+                    for k in (1, 0):
                         a_exit(i, r, k, "s")
                 a_quant(i, 0, 0, N)
             if n2:
@@ -380,7 +375,9 @@ def tile_rgat_pa_t_kernel(tc, adj, x, dmask, W, out):
             if not fin:
                 a_quant(i, 1, 0, N)
             if n1:
-                for k in range(0 if n2 else 2, 4):
+                for k in range(4):
+                    h_matmul(i + 1, 1, k)
+                for k in reversed(range(0 if n2 else 2, 4)):
                     h_exit(i + 1, 0, k, "s")
             if n2:
                 level(i + 2, 1, 0, NT)
@@ -391,6 +388,16 @@ def tile_rgat_pa_t_kernel(tc, adj, x, dmask, W, out):
             if n2:
                 level(i + 2, 3, 0, NT)
             if n1:
+                h_exit(i + 1, 1, 3, "v")
+            if n2:
+                level(i + 2, 4, 0, NT)
+            if n1:
+                h_quant(i + 1, 0)
+                norm(i + 1, 2, "v")
+                for k in (2, 1, 0):
+                    h_exit(i + 1, 1, k, "s")
+                norm(i + 1, 3, "v")
+                h_quant(i + 1, 1)
                 recip(i + 1, NV, NQ)
                 for q in range(NV, NQ):
                     norm(i + 1, q, "g")
@@ -400,31 +407,17 @@ def tile_rgat_pa_t_kernel(tc, adj, x, dmask, W, out):
             for t in range(NT):
                 relu0(i, t)
                 finish(i, t)
-                if n2 and t == 0:
-                    level(i + 2, 4, 0, NT)
                 if fin:
                     store(i, t, t + 1)
             if not fin:
                 store(i, 0, NT)
-            if n1:
-                for k in range(4):
-                    h_matmul(i + 1, 1, k)
-                for k in range(4):
-                    h_exit(i + 1, 1, k, "v" if k == 0 else "s")
             if n2:
                 x_transpose(i + 2)
                 x_exit(i + 2, 0, "v")
                 x_exit(i + 2, 1, "v")
-            if n1:
-                h_quant(i + 1, 0)
-                norm(i + 1, 2, "v")
             if i + 3 < B:
                 make_cap(i + 3)
             if n2:
                 x_quant(i + 2)
-            if n1:
-                norm(i + 1, 3, "v")
-                h_quant(i + 1, 1)
-            if n2:
                 for t in range(NT):
                     exps(i + 2, t)

@@ -16,7 +16,7 @@ B, N, H, R = 8, 512, 512, 2
 P = 128
 NT = N // P
 NQ = R * NT
-NV = 4
+NV = 3
 LAST = B - 1
 FLOPS = 2 * 2 * B * R * N * N * H
 
@@ -307,8 +307,8 @@ def tile_rgat_pa_t_kernel(tc, adj, x, dmask, W, out):
         exps(0, 2)
         exps(0, 3)
         make_cap(1)
-        mask(1, 0, 2)
         w_quant(1)
+        mask(1, 0, 2)
         for k in reversed(range(4)):
             h_exit(0, 0, k, "s")
         for k in range(4):
@@ -329,12 +329,14 @@ def tile_rgat_pa_t_kernel(tc, adj, x, dmask, W, out):
         x_exit(1, 0, "v")
         x_exit(1, 1, "v")
         h_quant(0, 0)
+        make_cap(2)
         x_quant(1)
         h_quant(0, 1)
-        make_cap(2)
 
-        for i in range(B):
-            n1, n2, fin = i + 1 < B, i + 2 < B, i == LAST
+        for i in range(LAST - 1):
+            nxt = i + 1
+            new = i + 2
+            v_banks = 1 + i % 2
             if i + 4 < B:
                 load_mask(i + 4, nc.sync)
                 load_a(i + 4, 0, NT)
@@ -343,81 +345,99 @@ def tile_rgat_pa_t_kernel(tc, adj, x, dmask, W, out):
             for r in range(R):
                 for k in range(2):
                     a_transpose(i, r, k)
-            if n1:
+            for r in range(R):
                 for k in range(4):
-                    h_matmul(i + 1, 0, k)
-            if n2:
-                mask(i + 2, 0, 2)
-            elif n1:
-                h_exit(i + 1, 0, 0, "v")
-                h_exit(i + 1, 0, 1, "v")
-            if n1:
-                recip(i + 1, 0, NV)
-            if n2:
-                mask(i + 2, 2, 4)
-            if fin:
-                a_exit(i, 0, 0, "s")
-                a_exit(i, 1, 0, "v")
-                a_exit(i, 0, 1, "s")
-                a_exit(i, 1, 1, "s")
-                for k in range(2):
-                    for r in range(R):
-                        a_quant(i, r, 256 * k, 256 * k + 256)
-            else:
-                for r in range(R):
-                    for k in (1, 0):
-                        a_exit(i, r, k, "s")
-                a_quant(i, 0, 0, N)
-            if n2:
-                level(i + 2, 0, 0, NT)
-            elif n1:
-                norm(i + 1, 0, "v")
-            if not fin:
-                a_quant(i, 1, 0, N)
-            if n1:
-                for k in range(4):
-                    h_matmul(i + 1, 1, k)
-                for k in reversed(range(0 if n2 else 2, 4)):
-                    h_exit(i + 1, 0, k, "s")
-            if n2:
-                level(i + 2, 1, 0, NT)
-                norm(i + 1, 0, "v")
-                level(i + 2, 2, 0, NT)
-            if n1:
-                norm(i + 1, 1, "v")
-            if n2:
-                level(i + 2, 3, 0, NT)
-            if n1:
-                h_exit(i + 1, 1, 3, "v")
-            if n2:
-                level(i + 2, 4, 0, NT)
-            if n1:
-                h_quant(i + 1, 0)
-                norm(i + 1, 2, "v")
-                for k in (2, 1, 0):
-                    h_exit(i + 1, 1, k, "s")
-                norm(i + 1, 3, "v")
-                h_quant(i + 1, 1)
-                recip(i + 1, NV, NQ)
-                for q in range(NV, NQ):
-                    norm(i + 1, q, "g")
+                    h_matmul(nxt, r, k)
+            mask(new, 0, 2)
+            recip(nxt, 0, NV)
+            mask(new, 2, 4)
+            for r in range(R):
+                for k in (1, 0):
+                    a_exit(i, r, k, "s")
+            a_quant(i, 0, 0, N)
+            level(new, 0, 0, NT)
+            a_quant(i, 1, 0, N)
+            for k in reversed(range(4)):
+                h_exit(nxt, 0, k, "s")
+            for k in reversed(range(4 - v_banks)):
+                h_exit(nxt, 1, k, "s")
+            level(new, 1, 0, NT)
+            norm(nxt, 0, "v")
+            level(new, 2, 0, NT)
+            norm(nxt, 1, "v")
+            level(new, 3, 0, NT)
+            norm(nxt, 2, "v")
+            h_quant(nxt, 0)
+            level(new, 4, 0, NT)
+            recip(nxt, NV, NQ)
+            for q in range(NV, NQ):
+                norm(nxt, q, "g")
+            for k in reversed(range(4 - v_banks, 4)):
+                h_exit(nxt, 1, k, "v")
             for r in range(R):
                 for t in range(NT):
                     g_matmul(i, t, r)
             for t in range(NT):
                 relu0(i, t)
                 finish(i, t)
-                if fin:
-                    store(i, t, t + 1)
-            if not fin:
-                store(i, 0, NT)
-            if n2:
-                x_transpose(i + 2)
-                x_exit(i + 2, 0, "v")
-                x_exit(i + 2, 1, "v")
-            if i + 3 < B:
+            store(i, 0, NT)
+            x_transpose(new)
+            x_exit(new, 0, "v")
+            x_exit(new, 1, "v")
+            h_quant(nxt, 1)
+            if new < LAST:
                 make_cap(i + 3)
-            if n2:
-                x_quant(i + 2)
-                for t in range(NT):
-                    exps(i + 2, t)
+            x_quant(new)
+            for t in range(NT):
+                exps(new, t)
+
+        i = LAST - 1
+        for r in range(R):
+            for k in range(2):
+                a_transpose(i, r, k)
+        for r in range(R):
+            for k in range(4):
+                h_matmul(LAST, r, k)
+        recip(LAST, 0, NQ)
+        for r in range(R):
+            for k in (1, 0):
+                a_exit(i, r, k, "s")
+        norm(LAST, 0, "v")
+        norm(LAST, 1, "v")
+        a_quant(i, 0, 0, N)
+        norm(LAST, 2, "v")
+        norm(LAST, 3, "v")
+        a_quant(i, 1, 0, N)
+        for q in range(4, NQ):
+            norm(LAST, q, "v")
+        for k in range(4):
+            h_exit(LAST, 0, k, "s")
+        h_exit(LAST, 1, 3, "v")
+        for k in reversed(range(3)):
+            h_exit(LAST, 1, k, "s")
+        for k in range(2):
+            for r in range(R):
+                a_transpose(LAST, r, k)
+        h_quant(LAST, 0)
+        a_exit(LAST, 1, 0, "v")
+        a_exit(LAST, 0, 0, "s")
+        a_exit(LAST, 0, 1, "s")
+        a_exit(LAST, 1, 1, "s")
+        h_quant(LAST, 1)
+        for k in range(2):
+            for r in range(R):
+                a_quant(LAST, r, 256 * k, 256 * k + 256)
+        for r in range(R):
+            for t in range(NT):
+                g_matmul(i, t, r)
+        for t in range(NT):
+            relu0(i, t)
+            finish(i, t)
+        store(i, 0, NT)
+        for t in range(NT):
+            for r in range(R):
+                g_matmul(LAST, t, r)
+        for t in range(NT):
+            relu0(LAST, t)
+            finish(LAST, t)
+            store(LAST, t, t + 1)

@@ -38,7 +38,9 @@ def tile_rgat_pa_t_kernel(tc, adj, x, dmask, W, out):
         st = [dict() for b in range(B)]
 
         ident = const.tile([P, P], F32)
+        ident_b = const.tile([P, P], BF16)
         dm = const.tile([P, B * N], BF16)
+        dm_col = const.tile([P, NT], BF16)
         w_codes = const.tile([P, R, H], U32, align_bytes=64)
         w_scales = const.tile([P, R, H], U8, align_bytes=64)
         w_stage = two.tile([P, 2, R, 4 * H], BF16, tag="e", align_bytes=64)
@@ -46,8 +48,16 @@ def tile_rgat_pa_t_kernel(tc, adj, x, dmask, W, out):
         w_grp = w_stage[:, 1]
         dm_row = dmask.rearrange("b o m -> (b o m)")
 
-        def load_mask(b, queue):
-            queue.dma_start(out=dm[:, N * b : N * b + N], in_=dm_row[N * b : N * b + N].partition_broadcast(P))
+        def load_mask(b):
+            nc.sync.dma_start(out=dm[:, N * b : N * b + N], in_=dm_row[N * b : N * b + N].partition_broadcast(P))
+
+        def spread_mask(b):
+            pm = banks.tile([P, NT, P], F32, tag="bank", name="pm")
+            for j in range(NT):
+                nc.tensor.matmul(
+                    pm[:, j, :], lhsT=dm_col[:, j : j + 1].to_broadcast([P, P]), rhs=ident_b[:], start=True, stop=True
+                )
+            st[b]["pm"] = pm
 
         def load_w(r):
             for u in range(2):
@@ -69,9 +79,13 @@ def tile_rgat_pa_t_kernel(tc, adj, x, dmask, W, out):
 
         def make_cap(b):
             cap = three.tile([P, N], F32, name="cap")
-            nc.vector.tensor_scalar(
-                out=cap[:], in0=dm[:, N * b : N * b + N], scalar1=OPEN, scalar2=SHUT, op0=ALU.mult, op1=ALU.add
-            )
+            if b == 0:
+                dst = cap[:].rearrange("p (m j) -> p m j", j=NT)
+                src = st[b]["pm"][:].rearrange("p j m -> p m j")
+            else:
+                dst = cap[:]
+                src = dm[:, N * b : N * b + N]
+            nc.vector.tensor_scalar(out=dst, in0=src, scalar1=OPEN, scalar2=SHUT, op0=ALU.mult, op1=ALU.add)
             st[b]["cap"] = cap
 
         def w_group(r, eng):
@@ -269,8 +283,9 @@ def tile_rgat_pa_t_kernel(tc, adj, x, dmask, W, out):
         def store(b, t0, t1):
             nc.sync.dma_start(out=out_v[b][:, t0:t1, :], in_=st[b]["ot"][:, t0:t1, :])
 
+        nc.scalar.dma_start(out=dm_col[:], in_=dmask[0].rearrange("o (p j) -> (o p) j", j=NT))
+        make_identity(nc, ident_b[:])
         make_identity(nc, ident[:])
-        load_mask(0, nc.scalar)
         load_a(0, 0, 1)
         load_a(0, 1, 2)
         load_x(0)
@@ -278,10 +293,11 @@ def tile_rgat_pa_t_kernel(tc, adj, x, dmask, W, out):
         load_a(0, 2, 4)
         load_w(1)
         for b in (1, 2, 3):
-            load_mask(b, nc.sync)
             load_a(b, 0, NT)
+            load_mask(b)
             if b < 3:
                 load_x(b)
+        spread_mask(0)
 
         def woven_tree(b, t):
             mask(b, t, t + 1)
@@ -338,7 +354,7 @@ def tile_rgat_pa_t_kernel(tc, adj, x, dmask, W, out):
             new = i + 2
             v_banks = 1 + i % 2
             if i + 4 < B:
-                load_mask(i + 4, nc.sync)
+                load_mask(i + 4)
                 load_a(i + 4, 0, NT)
             if i + 3 < B:
                 load_x(i + 3)

@@ -33,6 +33,7 @@ def tile_rgat_pa_t_kernel(tc, adj, x, dmask, W, out):
         two = ctx.enter_context(tc.tile_pool(name="two", bufs=2))
         three = ctx.enter_context(tc.tile_pool(name="three", bufs=3))
         four = ctx.enter_context(tc.tile_pool(name="four", bufs=4))
+        eight = ctx.enter_context(tc.tile_pool(name="eight", bufs=8))
         banks = ctx.enter_context(tc.psum_pool(name="banks", bufs=8))
 
         st = [dict() for b in range(B)]
@@ -262,26 +263,26 @@ def tile_rgat_pa_t_kernel(tc, adj, x, dmask, W, out):
             st[b]["g%d%d" % (t, r)] = g
 
         def relu0(b, t):
-            g0 = four.tile([P, H], F32, name="g0s")
+            g0 = eight.tile([P, H], F32, name="g0s")
             nc.scalar.activation(out=g0[:], in_=st[b]["g%d0" % t][:], func=ACT.Relu)
             st[b]["g0s%d" % t] = g0
 
-        def finish(b, t):
+        def finish(b, t, lo=0, hi=H):
             if "ot" not in st[b]:
                 st[b]["ot"] = two.tile([P, NT, H], F32, name="ot")
             nc.vector.scalar_tensor_tensor(
-                out=st[b]["ot"][:, t, :],
-                in0=st[b]["g%d1" % t][:],
+                out=st[b]["ot"][:, t, lo:hi],
+                in0=st[b]["g%d1" % t][:, lo:hi],
                 scalar=0.0,
-                in1=st[b]["g0s%d" % t][:],
+                in1=st[b]["g0s%d" % t][:, lo:hi],
                 op0=ALU.max,
                 op1=ALU.add,
             )
 
         out_v = [out[b].rearrange("(p t) o -> p t o", t=NT) for b in range(B)]
 
-        def store(b, t0, t1):
-            nc.sync.dma_start(out=out_v[b][:, t0:t1, :], in_=st[b]["ot"][:, t0:t1, :])
+        def store(b, t0, t1, lo=0, hi=H):
+            nc.sync.dma_start(out=out_v[b][:, t0:t1, lo:hi], in_=st[b]["ot"][:, t0:t1, lo:hi])
 
         nc.scalar.dma_start(out=dm_col[:], in_=dmask[0].rearrange("o (p j) -> (o p) j", j=NT))
         make_identity(nc, ident_b[:])
@@ -333,15 +334,17 @@ def tile_rgat_pa_t_kernel(tc, adj, x, dmask, W, out):
         for k in reversed(range(4)):
             h_exit(0, 1, k, "s")
         mask(1, 2, 4)
-        recip(0, 0, NQ)
+        recip(0, 0, NQ - 1)
         for j in range(5):
             level(1, j, 0, NT)
             if j < 4:
                 norm(0, j, "v")
         for t in range(NT):
             exps(1, t)
-        for q in range(4, NQ):
+        for q in range(4, NQ - 1):
             norm(0, q, "v")
+        recip(0, NQ - 1, NQ)
+        norm(0, NQ - 1, "g")
         x_exit(1, 0, "v")
         x_exit(1, 1, "v")
         h_quant(0, 0)
@@ -384,8 +387,10 @@ def tile_rgat_pa_t_kernel(tc, adj, x, dmask, W, out):
             level(new, 3, 0, NT)
             norm(nxt, 2, "v")
             h_quant(nxt, 0)
-            level(new, 4, 0, NT)
+            if new < LAST:
+                make_cap(i + 3)
             recip(nxt, NV, NQ)
+            level(new, 4, 0, NT)
             for q in range(NV, NQ):
                 norm(nxt, q, "g")
             for k in reversed(range(4 - v_banks, 4)):
@@ -401,8 +406,6 @@ def tile_rgat_pa_t_kernel(tc, adj, x, dmask, W, out):
             x_exit(new, 0, "v")
             x_exit(new, 1, "v")
             h_quant(nxt, 1)
-            if new < LAST:
-                make_cap(i + 3)
             x_quant(new)
             for t in range(NT):
                 exps(new, t)
@@ -455,5 +458,7 @@ def tile_rgat_pa_t_kernel(tc, adj, x, dmask, W, out):
                 g_matmul(LAST, t, r)
         for t in range(NT):
             relu0(LAST, t)
-            finish(LAST, t)
-            store(LAST, t, t + 1)
+            for c in range(0, H, H // 2 if t == NT - 1 else H):
+                d = c + H // 2 if t == NT - 1 else H
+                finish(LAST, t, c, d)
+                store(LAST, t, t + 1, c, d)

@@ -27,7 +27,6 @@ SHUT = -1.004922760984937e30
 def tile_rgat_pa_t_kernel(tc, adj, x, dmask, W, out):
     nc = tc.nc
     with ExitStack() as ctx:
-        ctx.enter_context(tc.manual_schedule())
         const = ctx.enter_context(tc.tile_pool(name="const", bufs=1))
         one = ctx.enter_context(tc.tile_pool(name="one", bufs=1))
         two = ctx.enter_context(tc.tile_pool(name="two", bufs=2))
@@ -284,117 +283,171 @@ def tile_rgat_pa_t_kernel(tc, adj, x, dmask, W, out):
         def store(b, t0, t1, lo=0, hi=H):
             nc.sync.dma_start(out=out_v[b][:, t0:t1, lo:hi], in_=st[b]["ot"][:, t0:t1, lo:hi])
 
-        nc.scalar.dma_start(out=dm_col[:], in_=dmask[0].rearrange("o (p j) -> (o p) j", j=NT))
-        make_identity(nc, ident_b[:])
-        make_identity(nc, ident[:])
-        load_a(0, 0, 1)
-        load_a(0, 1, 2)
-        load_x(0)
-        load_w(0)
-        load_a(0, 2, 4)
-        load_w(1)
-        for b in (1, 2, 3):
-            load_a(b, 0, NT)
-            load_mask(b)
-            if b < 3:
-                load_x(b)
-        spread_mask(0)
+        with tc.manual_schedule():
+            nc.scalar.dma_start(out=dm_col[:], in_=dmask[0].rearrange("o (p j) -> (o p) j", j=NT))
+            make_identity(nc, ident_b[:])
+            make_identity(nc, ident[:])
+            load_a(0, 0, 1)
+            load_a(0, 1, 2)
+            load_x(0)
+            load_w(0)
+            load_a(0, 2, 4)
+            load_w(1)
+            for b in (1, 2, 3):
+                load_a(b, 0, NT)
+                load_mask(b)
+                if b < 3:
+                    load_x(b)
+            spread_mask(0)
 
-        def woven_tree(b, t):
-            mask(b, t, t + 1)
-            mask(b, t + 1, t + 2)
+            def woven_tree(b, t):
+                mask(b, t, t + 1)
+                mask(b, t + 1, t + 2)
+                for j in range(5):
+                    level(b, j, t, t + 1)
+                    level(b, j, t + 1, t + 2)
+
+            make_cap(0)
+            woven_tree(0, 0)
+            x_transpose(0)
+            x_exit(0, 0, "s")
+            x_exit(0, 1, "s")
+            exps(0, 0)
+            exps(0, 1)
+            w_group(0, "v")
+            w_group(1, "s")
+            x_quant(0)
+            w_quant(0)
+            for k in range(4):
+                h_matmul(0, 0, k)
+            woven_tree(0, 2)
+            exps(0, 2)
+            exps(0, 3)
+            make_cap(1)
+            w_quant(1)
+            mask(1, 0, 2)
+            for k in reversed(range(4)):
+                h_exit(0, 0, k, "s")
+            for k in range(4):
+                h_matmul(0, 1, k)
+            x_transpose(1)
+            for k in reversed(range(4)):
+                h_exit(0, 1, k, "s")
+            mask(1, 2, 4)
+            recip(0, 0, NQ - 1)
             for j in range(5):
-                level(b, j, t, t + 1)
-                level(b, j, t + 1, t + 2)
+                level(1, j, 0, NT)
+                if j < 4:
+                    norm(0, j, "v")
+            for t in range(NT):
+                exps(1, t)
+            for q in range(4, NQ - 1):
+                norm(0, q, "v")
+            recip(0, NQ - 1, NQ)
+            norm(0, NQ - 1, "g")
+            x_exit(1, 0, "v")
+            x_exit(1, 1, "v")
+            h_quant(0, 0)
+            make_cap(2)
+            x_quant(1)
+            h_quant(0, 1)
 
-        make_cap(0)
-        woven_tree(0, 0)
-        x_transpose(0)
-        x_exit(0, 0, "s")
-        x_exit(0, 1, "s")
-        exps(0, 0)
-        exps(0, 1)
-        w_group(0, "v")
-        w_group(1, "s")
-        x_quant(0)
-        w_quant(0)
-        for k in range(4):
-            h_matmul(0, 0, k)
-        woven_tree(0, 2)
-        exps(0, 2)
-        exps(0, 3)
-        make_cap(1)
-        w_quant(1)
-        mask(1, 0, 2)
-        for k in reversed(range(4)):
-            h_exit(0, 0, k, "s")
-        for k in range(4):
-            h_matmul(0, 1, k)
-        x_transpose(1)
-        for k in reversed(range(4)):
-            h_exit(0, 1, k, "s")
-        mask(1, 2, 4)
-        recip(0, 0, NQ - 1)
-        for j in range(5):
-            level(1, j, 0, NT)
-            if j < 4:
-                norm(0, j, "v")
-        for t in range(NT):
-            exps(1, t)
-        for q in range(4, NQ - 1):
-            norm(0, q, "v")
-        recip(0, NQ - 1, NQ)
-        norm(0, NQ - 1, "g")
-        x_exit(1, 0, "v")
-        x_exit(1, 1, "v")
-        h_quant(0, 0)
-        make_cap(2)
-        x_quant(1)
-        h_quant(0, 1)
+        with tc.manual_schedule(
+            engines={mybir.EngineType.PE, mybir.EngineType.DVE, mybir.EngineType.SP, mybir.EngineType.Pool}
+        ):
+            for i in range(LAST - 1):
+                nxt = i + 1
+                new = i + 2
+                v_banks = 1 + i % 2
+                if i + 4 < B:
+                    load_mask(i + 4)
+                    load_a(i + 4, 0, NT)
+                if i + 3 < B:
+                    load_x(i + 3)
+                for r in range(R):
+                    for k in range(2):
+                        a_transpose(i, r, k)
+                for r in range(R):
+                    for k in range(4):
+                        h_matmul(nxt, r, k)
+                mask(new, 0, NT)
+                recip(nxt, 0, NV)
+                for r in range(R):
+                    for k in (1, 0):
+                        a_exit(i, r, k, "s")
+                a_quant(i, 0, 0, N)
+                level(new, 0, 0, NT)
+                a_quant(i, 1, 0, N)
+                for k in reversed(range(4)):
+                    h_exit(nxt, 0, k, "s")
+                for k in reversed(range(4 - v_banks)):
+                    h_exit(nxt, 1, k, "s")
+                level(new, 1, 0, NT)
+                norm(nxt, 0, "v")
+                level(new, 2, 0, NT)
+                norm(nxt, 1, "v")
+                level(new, 3, 0, NT)
+                norm(nxt, 2, "v")
+                h_quant(nxt, 0)
+                recip(nxt, NV, NQ)
+                if new < LAST:
+                    make_cap(i + 3)
+                level(new, 4, 0, NT)
+                for q in range(NV, NQ):
+                    norm(nxt, q, "g")
+                for k in reversed(range(4 - v_banks, 4)):
+                    h_exit(nxt, 1, k, "v")
+                for r in range(R):
+                    for t in range(NT):
+                        g_matmul(i, t, r)
+                for t in range(NT):
+                    relu0(i, t)
+                    finish(i, t)
+                store(i, 0, NT)
+                x_transpose(new)
+                x_exit(new, 0, "v")
+                x_exit(new, 1, "v")
+                h_quant(nxt, 1)
+                x_quant(new)
+                for t in range(NT):
+                    exps(new, t)
 
-        for i in range(LAST - 1):
-            nxt = i + 1
-            new = i + 2
-            v_banks = 1 + i % 2
-            if i + 4 < B:
-                load_mask(i + 4)
-                load_a(i + 4, 0, NT)
-            if i + 3 < B:
-                load_x(i + 3)
+            i = LAST - 1
             for r in range(R):
                 for k in range(2):
                     a_transpose(i, r, k)
             for r in range(R):
                 for k in range(4):
-                    h_matmul(nxt, r, k)
-            mask(new, 0, 2)
-            recip(nxt, 0, NV)
-            mask(new, 2, 4)
+                    h_matmul(LAST, r, k)
+            recip(LAST, 0, NQ)
             for r in range(R):
                 for k in (1, 0):
                     a_exit(i, r, k, "s")
+            norm(LAST, 0, "v")
+            norm(LAST, 1, "v")
             a_quant(i, 0, 0, N)
-            level(new, 0, 0, NT)
+            norm(LAST, 2, "v")
+            norm(LAST, 3, "v")
             a_quant(i, 1, 0, N)
-            for k in reversed(range(4)):
-                h_exit(nxt, 0, k, "s")
-            for k in reversed(range(4 - v_banks)):
-                h_exit(nxt, 1, k, "s")
-            level(new, 1, 0, NT)
-            norm(nxt, 0, "v")
-            level(new, 2, 0, NT)
-            norm(nxt, 1, "v")
-            level(new, 3, 0, NT)
-            norm(nxt, 2, "v")
-            h_quant(nxt, 0)
-            if new < LAST:
-                make_cap(i + 3)
-            recip(nxt, NV, NQ)
-            level(new, 4, 0, NT)
-            for q in range(NV, NQ):
-                norm(nxt, q, "g")
-            for k in reversed(range(4 - v_banks, 4)):
-                h_exit(nxt, 1, k, "v")
+            for q in range(4, NQ):
+                norm(LAST, q, "v")
+            for k in range(4):
+                h_exit(LAST, 0, k, "s")
+            h_exit(LAST, 1, 3, "v")
+            for k in reversed(range(3)):
+                h_exit(LAST, 1, k, "s")
+            for k in range(2):
+                for r in range(R):
+                    a_transpose(LAST, r, k)
+            h_quant(LAST, 0)
+            a_exit(LAST, 1, 0, "v")
+            a_exit(LAST, 0, 0, "s")
+            a_exit(LAST, 0, 1, "s")
+            a_exit(LAST, 1, 1, "s")
+            h_quant(LAST, 1)
+            for k in range(2):
+                for r in range(R):
+                    a_quant(LAST, r, 256 * k, 256 * k + 256)
             for r in range(R):
                 for t in range(NT):
                     g_matmul(i, t, r)
@@ -402,63 +455,12 @@ def tile_rgat_pa_t_kernel(tc, adj, x, dmask, W, out):
                 relu0(i, t)
                 finish(i, t)
             store(i, 0, NT)
-            x_transpose(new)
-            x_exit(new, 0, "v")
-            x_exit(new, 1, "v")
-            h_quant(nxt, 1)
-            x_quant(new)
             for t in range(NT):
-                exps(new, t)
-
-        i = LAST - 1
-        for r in range(R):
-            for k in range(2):
-                a_transpose(i, r, k)
-        for r in range(R):
-            for k in range(4):
-                h_matmul(LAST, r, k)
-        recip(LAST, 0, NQ)
-        for r in range(R):
-            for k in (1, 0):
-                a_exit(i, r, k, "s")
-        norm(LAST, 0, "v")
-        norm(LAST, 1, "v")
-        a_quant(i, 0, 0, N)
-        norm(LAST, 2, "v")
-        norm(LAST, 3, "v")
-        a_quant(i, 1, 0, N)
-        for q in range(4, NQ):
-            norm(LAST, q, "v")
-        for k in range(4):
-            h_exit(LAST, 0, k, "s")
-        h_exit(LAST, 1, 3, "v")
-        for k in reversed(range(3)):
-            h_exit(LAST, 1, k, "s")
-        for k in range(2):
-            for r in range(R):
-                a_transpose(LAST, r, k)
-        h_quant(LAST, 0)
-        a_exit(LAST, 1, 0, "v")
-        a_exit(LAST, 0, 0, "s")
-        a_exit(LAST, 0, 1, "s")
-        a_exit(LAST, 1, 1, "s")
-        h_quant(LAST, 1)
-        for k in range(2):
-            for r in range(R):
-                a_quant(LAST, r, 256 * k, 256 * k + 256)
-        for r in range(R):
+                for r in range(R):
+                    g_matmul(LAST, t, r)
             for t in range(NT):
-                g_matmul(i, t, r)
-        for t in range(NT):
-            relu0(i, t)
-            finish(i, t)
-        store(i, 0, NT)
-        for t in range(NT):
-            for r in range(R):
-                g_matmul(LAST, t, r)
-        for t in range(NT):
-            relu0(LAST, t)
-            for c in range(0, H, H // 2 if t == NT - 1 else H):
-                d = c + H // 2 if t == NT - 1 else H
-                finish(LAST, t, c, d)
-                store(LAST, t, t + 1, c, d)
+                relu0(LAST, t)
+                for c in range(0, H, H // 2 if t == NT - 1 else H):
+                    d = c + H // 2 if t == NT - 1 else H
+                    finish(LAST, t, c, d)
+                    store(LAST, t, t + 1, c, d)

from contextlib import ExitStack

import concourse.mybir as mybir
from concourse.masks import make_identity

F32 = mybir.dt.float32
BF16 = mybir.dt.bfloat16
U32 = mybir.dt.uint32
U8 = mybir.dt.uint8
FP8X4 = mybir.dt.float8_e4m3fn_x4
ALU = mybir.AluOpType
ACT = mybir.ActivationFunctionType
AX = mybir.AxisListType

B, N, H, R = 8, 512, 512, 2
P = 128
NT = N // P
NQ = R * NT
NV = 3
LAST = B - 1
FLOPS = 2 * 2 * B * R * N * N * H

OPEN = 3.3961513649220713e38
SHUT = -1.004922760984937e30


def tile_rgat_pa_t_kernel(tc, adj, x, dmask, W, out):
    nc = tc.nc
    with ExitStack() as ctx:
        const = ctx.enter_context(tc.tile_pool(name="const", bufs=1))
        one = ctx.enter_context(tc.tile_pool(name="one", bufs=1))
        two = ctx.enter_context(tc.tile_pool(name="two", bufs=2))
        three = ctx.enter_context(tc.tile_pool(name="three", bufs=3))
        four = ctx.enter_context(tc.tile_pool(name="four", bufs=4))
        eight = ctx.enter_context(tc.tile_pool(name="eight", bufs=8))
        banks = ctx.enter_context(tc.psum_pool(name="banks", bufs=8))

        st = [dict() for b in range(B)]

        ident = const.tile([P, P], F32)
        ident_b = const.tile([P, P], BF16)
        dm = const.tile([P, B * N], BF16)
        dm_col = const.tile([P, NT], BF16)
        w_codes = const.tile([P, R, H], U32, align_bytes=64)
        w_scales = const.tile([P, R, H], U8, align_bytes=64)
        w_stage = two.tile([P, 2, R, 4 * H], BF16, tag="e", align_bytes=64)
        w_raw = w_stage[:, 0]
        w_grp = w_stage[:, 1]
        dm_row = dmask.rearrange("b o m -> (b o m)")

        def load_mask(b):
            nc.sync.dma_start(out=dm[:, N * b : N * b + N], in_=dm_row[N * b : N * b + N].partition_broadcast(P))

        def spread_mask(b):
            pm = banks.tile([P, NT, P], F32, tag="bank", name="pm")
            for j in range(NT):
                nc.tensor.matmul(
                    pm[:, j, :], lhsT=dm_col[:, j : j + 1].to_broadcast([P, P]), rhs=ident_b[:], start=True, stop=True
                )
            st[b]["pm"] = pm

        def load_w(r):
            for u in range(2):
                nc.sync.dma_start(
                    out=w_raw[:, r, 1024 * u : 1024 * u + 1024],
                    in_=W[r, 256 * u : 256 * u + 256, :].rearrange("(q e) o -> q (e o)", e=2),
                )

        def load_x(b):
            xs = three.tile([P, 2, 2 * H], BF16, name="xs")
            nc.sync.dma_start(out=xs[:], in_=x[b].rearrange("(u p e) f -> p u (e f)", u=2, e=2))
            st[b]["xs"] = xs

        def load_a(b, t0, t1):
            if t0 == 0:
                st[b]["a"] = four.tile([P, NT, N * R], BF16, name="a")
            src = adj[b].rearrange("(p t) m r -> p t (m r)", t=NT)
            nc.sync.dma_start(out=st[b]["a"][:, t0:t1, :], in_=src[:, t0:t1, :])

        def make_cap(b):
            cap = three.tile([P, N], F32, name="cap")
            if b == 0:
                dst = cap[:].rearrange("p (m j) -> p m j", j=NT)
                src = st[b]["pm"][:].rearrange("p j m -> p m j")
            else:
                dst = cap[:]
                src = dm[:, N * b : N * b + N]
            nc.vector.tensor_scalar(out=dst, in0=src, scalar1=OPEN, scalar2=SHUT, op0=ALU.mult, op1=ALU.add)
            st[b]["cap"] = cap

        def w_group(r, eng):
            src = w_raw[:, r].rearrange("p (t c i) -> p c t i", t=4, i=4)
            dst = w_grp[:, r].rearrange("p (c i t) -> p c t i", i=4, t=4)
            if eng == "v":
                nc.vector.tensor_copy(out=dst, in_=src)
            else:
                nc.scalar.copy(out=dst, in_=src)

        def w_quant(r):
            nc.vector.quantize_mx(out=w_codes[:, r, :].bitcast(FP8X4), scales=w_scales[:, r, :], in_=w_grp[:, r])

        def words_exit(dst, bank, eng):
            src = bank[:].rearrange("p u n -> p n u")
            if eng == "v":
                nc.vector.tensor_copy(out=dst, in_=src)
            else:
                nc.scalar.copy(out=dst, in_=src)

        def x_transpose(b):
            st[b]["xt"] = []
            for uu in range(2):
                xt = banks.tile([P, 2, 256], F32, tag="bank", name="xt")
                for e in range(2):
                    xw = st[b]["xs"][:, uu, H * e : H * e + H].bitcast(F32)
                    for u in range(2):
                        nc.tensor.transpose(xt[:, u, P * e : P * e + P], xw[:, P * u : P * u + P], ident[:])
                st[b]["xt"].append(xt)

        def x_exit(b, k, eng):
            if "xg" not in st[b]:
                st[b]["xg"] = two.tile([P, N * 4], BF16, align_bytes=64, name="xg")
            dst = st[b]["xg"][:].bitcast(F32).rearrange("p (n u) -> p n u", u=2)[:, 256 * k : 256 * k + 256, :]
            words_exit(dst, st[b]["xt"][k], eng)

        def x_quant(b):
            x_codes = two.tile([P, N], U32, align_bytes=64, name="x_codes")
            x_scales = two.tile([P, N], U8, align_bytes=64, name="x_scales")
            nc.vector.quantize_mx(out=x_codes[:].bitcast(FP8X4), scales=x_scales[:], in_=st[b]["xg"][:])
            st[b]["xc"] = (x_codes, x_scales)

        def mask(b, t0, t1):
            nc.vector.tensor_tensor(
                out=st[b]["a"][:, t0:t1, :],
                in0=st[b]["a"][:, t0:t1, :],
                in1=st[b]["cap"][:].bitcast(BF16).unsqueeze(1).to_broadcast([P, t1 - t0, N * R]),
                op=ALU.min,
            )

        def level(b, j, t0, t1):
            key = "lv%d" % t0
            if "nmx" not in st[b]:
                st[b]["nmx"] = three.tile([P, NT, R], F32, name="nmx")
            cur = st[b]["a"][:, t0:t1, :] if j == 0 else st[b][key]
            if j < 4:
                width = 512 // (2 ** j)
                nxt = one.tile([P, t1 - t0, width], BF16, name="tree%d_%d" % (width, NT if t1 - t0 == NT else t0 % 2))
                nc.vector.tensor_tensor(out=nxt[:], in0=cur[:, :, 0:width], in1=cur[:, :, width : 2 * width], op=ALU.max)
                st[b][key] = nxt[:]
            else:
                nc.vector.tensor_reduce(
                    out=st[b]["nmx"][:, t0:t1, :],
                    in_=cur.rearrange("p t (m r) -> p t r m", r=R),
                    axis=AX.X,
                    op=ALU.max,
                    negate=True,
                )

        def exps(b, t):
            if t == 0:
                st[b]["e"] = two.tile([P, NT, R, N], F32, tag="e", name="e", align_bytes=64)
                st[b]["ssum"] = three.tile([P, R * NT], F32, name="ssum")
                st[b]["att"] = two.tile([P, R, NT, N], BF16, name="att")
            row = st[b]["a"][:, t, :].rearrange("p (m r) -> p m r", r=R)
            for r in range(R):
                nc.scalar.activation(
                    out=st[b]["e"][:, t, r, :],
                    in_=row[:, :, r],
                    func=ACT.Exp,
                    bias=st[b]["nmx"][:, t, r : r + 1],
                    scale=1.0,
                    accum_out=st[b]["ssum"][:, NT * r + t : NT * r + t + 1],
                )

        def recip(b, lo, hi):
            rs = three.tile([P, R * NT], F32, name="rs%d" % lo)
            nc.vector.reciprocal(out=rs[:, lo:hi], in_=st[b]["ssum"][:, lo:hi])
            for q in range(lo, hi):
                st[b]["rs%d" % q] = rs

        def norm(b, q, eng):
            r, t = q // NT, q % NT
            dst = st[b]["att"][:, r, t, :]
            src = st[b]["e"][:, t, r, :]
            scale = st[b]["rs%d" % q][:, q : q + 1]
            if eng == "v":
                nc.vector.tensor_scalar(out=dst, in0=src, scalar1=scale, scalar2=None, op0=ALU.mult)
            else:
                nc.gpsimd.tensor_scalar(out=dst, in0=src, scalar1=scale, scalar2=0.0, op0=ALU.mult, op1=ALU.add)

        def a_transpose(b, r, k):
            pt = banks.tile([P, 2, 256], F32, tag="bank", name="pt")
            for tt in range(2):
                aw = st[b]["att"][:, r, 2 * k + tt, :].bitcast(F32)
                for u in range(2):
                    nc.tensor.transpose(pt[:, u, P * tt : P * tt + P], aw[:, P * u : P * u + P], ident[:])
            st[b]["pt%d%d" % (r, k)] = pt

        def a_exit(b, r, k, eng):
            key = "ag%d" % r
            if key not in st[b]:
                st[b][key] = two.tile([P, N * 4], BF16, align_bytes=64, name=key)
            dst = st[b][key][:].bitcast(F32).rearrange("p (n u) -> p n u", u=2)[:, 256 * k : 256 * k + 256, :]
            words_exit(dst, st[b]["pt%d%d" % (r, k)], eng)

        def a_quant(b, r, lo, hi):
            if lo == 0:
                codes = two.tile([P, N], U32, align_bytes=64, name="a_codes%d" % r)
                scales = two.tile([P, N], U8, align_bytes=64, name="a_scales%d" % r)
                st[b]["ac%d" % r] = (codes, scales)
            codes, scales = st[b]["ac%d" % r]
            nc.vector.quantize_mx(
                out=codes[:, lo:hi].bitcast(FP8X4), scales=scales[:, lo:hi], in_=st[b]["ag%d" % r][:, 4 * lo : 4 * hi]
            )

        def h_matmul(b, r, og):
            ph = banks.tile([P, NT, P], F32, tag="bank", name="ph")
            x_codes, x_scales = st[b]["xc"]
            for c in range(NT):
                nc.tensor.matmul_mx(
                    out=ph[:, c, :],
                    lhsT=x_codes[:, P * c : P * c + P].bitcast(FP8X4),
                    lhsT_scale=x_scales[:, P * c : P * c + P],
                    rhs=w_codes[:, r, P * og : P * og + P].bitcast(FP8X4),
                    rhs_scale=w_scales[:, r, P * og : P * og + P],
                    start=True,
                    stop=True,
                )
            st[b]["ph%d%d" % (r, og)] = ph

        def h_exit(b, r, og, eng):
            key = "hg%d" % r
            if key not in st[b]:
                st[b][key] = two.tile([P, H, 4], BF16, align_bytes=64, name=key)
            dst = st[b][key][:, P * og : P * og + P, :]
            src = st[b]["ph%d%d" % (r, og)][:].rearrange("p c o -> p o c")
            if eng == "v":
                nc.vector.tensor_copy(out=dst, in_=src)
            else:
                nc.scalar.copy(out=dst, in_=src)

        def h_quant(b, r):
            codes = two.tile([P, H], U32, align_bytes=64, name="h_codes%d" % r)
            scales = two.tile([P, H], U8, align_bytes=64, name="h_scales%d" % r)
            nc.vector.quantize_mx(
                out=codes[:].bitcast(FP8X4), scales=scales[:], in_=st[b]["hg%d" % r][:].rearrange("p o c -> p (o c)")
            )
            st[b]["hc%d" % r] = (codes, scales)

        def g_matmul(b, t, r):
            g = banks.tile([P, H], F32, tag="bank", name="g%d" % r)
            a_codes, a_scales = st[b]["ac%d" % r]
            h_codes, h_scales = st[b]["hc%d" % r]
            nc.tensor.matmul_mx(
                out=g[:],
                lhsT=a_codes[:, P * t : P * t + P].bitcast(FP8X4),
                lhsT_scale=a_scales[:, P * t : P * t + P],
                rhs=h_codes[:].bitcast(FP8X4),
                rhs_scale=h_scales[:],
                start=True,
                stop=True,
            )
            st[b]["g%d%d" % (t, r)] = g

        def relu0(b, t):
            g0 = eight.tile([P, H], F32, name="g0s")
            nc.scalar.activation(out=g0[:], in_=st[b]["g%d0" % t][:], func=ACT.Relu)
            st[b]["g0s%d" % t] = g0

        def finish(b, t, lo=0, hi=H):
            if "ot" not in st[b]:
                st[b]["ot"] = two.tile([P, NT, H], F32, name="ot")
            nc.vector.scalar_tensor_tensor(
                out=st[b]["ot"][:, t, lo:hi],
                in0=st[b]["g%d1" % t][:, lo:hi],
                scalar=0.0,
                in1=st[b]["g0s%d" % t][:, lo:hi],
                op0=ALU.max,
                op1=ALU.add,
            )

        out_v = [out[b].rearrange("(p t) o -> p t o", t=NT) for b in range(B)]

        def store(b, t0, t1, lo=0, hi=H):
            nc.sync.dma_start(out=out_v[b][:, t0:t1, lo:hi], in_=st[b]["ot"][:, t0:t1, lo:hi])

        with tc.manual_schedule():
            nc.scalar.dma_start(out=dm_col[:], in_=dmask[0].rearrange("o (p j) -> (o p) j", j=NT))
            make_identity(nc, ident_b[:])
            make_identity(nc, ident[:])
            load_a(0, 0, 1)
            load_a(0, 1, 2)
            load_x(0)
            load_w(0)
            load_a(0, 2, 4)
            load_w(1)
            for b in (1, 2, 3):
                load_a(b, 0, NT)
                load_mask(b)
                if b < 3:
                    load_x(b)
            spread_mask(0)

            def woven_tree(b, t):
                mask(b, t, t + 1)
                mask(b, t + 1, t + 2)
                for j in range(5):
                    level(b, j, t, t + 1)
                    level(b, j, t + 1, t + 2)

            make_cap(0)
            woven_tree(0, 0)
            x_transpose(0)
            x_exit(0, 0, "s")
            x_exit(0, 1, "s")
            exps(0, 0)
            exps(0, 1)
            w_group(0, "v")
            w_group(1, "s")
            x_quant(0)
            w_quant(0)
            for k in range(4):
                h_matmul(0, 0, k)
            woven_tree(0, 2)
            exps(0, 2)
            exps(0, 3)
            make_cap(1)
            w_quant(1)
            mask(1, 0, 2)
            for k in reversed(range(4)):
                h_exit(0, 0, k, "s")
            for k in range(4):
                h_matmul(0, 1, k)
            x_transpose(1)
            for k in reversed(range(4)):
                h_exit(0, 1, k, "s")
            mask(1, 2, 4)
            recip(0, 0, NQ - 1)
            for j in range(5):
                level(1, j, 0, NT)
                if j < 4:
                    norm(0, j, "v")
            for t in range(NT):
                exps(1, t)
            for q in range(4, NQ - 1):
                norm(0, q, "v")
            recip(0, NQ - 1, NQ)
            norm(0, NQ - 1, "g")
            x_exit(1, 0, "v")
            x_exit(1, 1, "v")
            h_quant(0, 0)
            make_cap(2)
            x_quant(1)
            h_quant(0, 1)

        with tc.manual_schedule(
            engines={mybir.EngineType.PE, mybir.EngineType.DVE, mybir.EngineType.SP, mybir.EngineType.Pool}
        ):
            for i in range(LAST - 1):
                nxt = i + 1
                new = i + 2
                v_banks = 1 + i % 2
                if i + 4 < B:
                    load_mask(i + 4)
                    load_a(i + 4, 0, NT)
                if i + 3 < B:
                    load_x(i + 3)
                for r in range(R):
                    for k in range(2):
                        a_transpose(i, r, k)
                for r in range(R):
                    for k in range(4):
                        h_matmul(nxt, r, k)
                mask(new, 0, NT)
                recip(nxt, 0, NV)
                for r in range(R):
                    for k in (1, 0):
                        a_exit(i, r, k, "s")
                a_quant(i, 0, 0, N)
                level(new, 0, 0, NT)
                a_quant(i, 1, 0, N)
                for k in reversed(range(4)):
                    h_exit(nxt, 0, k, "s")
                for k in reversed(range(4 - v_banks)):
                    h_exit(nxt, 1, k, "s")
                level(new, 1, 0, NT)
                norm(nxt, 0, "v")
                level(new, 2, 0, NT)
                norm(nxt, 1, "v")
                level(new, 3, 0, NT)
                norm(nxt, 2, "v")
                h_quant(nxt, 0)
                recip(nxt, NV, NQ)
                if new < LAST:
                    make_cap(i + 3)
                level(new, 4, 0, NT)
                for q in range(NV, NQ):
                    norm(nxt, q, "g")
                for k in reversed(range(4 - v_banks, 4)):
                    h_exit(nxt, 1, k, "v")
                for r in range(R):
                    for t in range(NT):
                        g_matmul(i, t, r)
                for t in range(NT):
                    relu0(i, t)
                    finish(i, t)
                store(i, 0, NT)
                x_transpose(new)
                x_exit(new, 0, "v")
                x_exit(new, 1, "v")
                h_quant(nxt, 1)
                x_quant(new)
                for t in range(NT):
                    exps(new, t)

            i = LAST - 1
            for r in range(R):
                for k in range(2):
                    a_transpose(i, r, k)
            for r in range(R):
                for k in range(4):
                    h_matmul(LAST, r, k)
            recip(LAST, 0, NQ)
            for r in range(R):
                for k in (1, 0):
                    a_exit(i, r, k, "s")
            norm(LAST, 0, "v")
            norm(LAST, 1, "v")
            a_quant(i, 0, 0, N)
            norm(LAST, 2, "v")
            norm(LAST, 3, "v")
            a_quant(i, 1, 0, N)
            for q in range(4, NQ):
                norm(LAST, q, "v")
            for k in range(4):
                h_exit(LAST, 0, k, "s")
            h_exit(LAST, 1, 3, "v")
            for k in reversed(range(3)):
                h_exit(LAST, 1, k, "s")
            for k in range(2):
                for r in range(R):
                    a_transpose(LAST, r, k)
            h_quant(LAST, 0)
            a_exit(LAST, 1, 0, "v")
            a_exit(LAST, 0, 0, "s")
            a_exit(LAST, 0, 1, "s")
            a_exit(LAST, 1, 1, "s")
            h_quant(LAST, 1)
            for k in range(2):
                for r in range(R):
                    a_quant(LAST, r, 256 * k, 256 * k + 256)
            for r in range(R):
                for t in range(NT):
                    g_matmul(i, t, r)
            for t in range(NT):
                relu0(i, t)
                finish(i, t)
            store(i, 0, NT)
            for t in range(NT):
                for r in range(R):
                    g_matmul(LAST, t, r)
            for t in range(NT):
                relu0(LAST, t)
                for c in range(0, H, H // 2 if t == NT - 1 else H):
                    d = c + H // 2 if t == NT - 1 else H
                    finish(LAST, t, c, d)
                    store(LAST, t, t + 1, c, d)
